import numpy as np
import ml_dtypes


def mxq(x, axis, fmt="e4m3"):
    dtype, down = {"e4m3": (ml_dtypes.float8_e4m3fn, 7), "e5m2": (ml_dtypes.float8_e5m2, 14)}[fmt]
    v = np.moveaxis(np.asarray(x, np.float32).astype(ml_dtypes.bfloat16).astype(np.float64), axis, -1)
    blocks = v.reshape(v.shape[:-1] + (-1, 32))
    amax = np.abs(blocks).max(-1, keepdims=True)
    byte = np.maximum(np.where(amax > 0, np.frexp(amax)[1] - 1 + 127, 0) - down, 1)
    scale = np.exp2(byte - 127.0)
    codes = (blocks / scale).astype(np.float32).astype(dtype).astype(np.float64)
    return np.moveaxis((codes * scale).reshape(v.shape), -1, axis)


WIDE = False


def mx_kscale(k):
    if not WIDE:
        return np.ones(k)
    levels = np.array([10, -10, 5, -5, 0])
    a = np.random.permutation(np.resize(levels, k // 512 * 4)).reshape(k // 512, 4)
    idx = np.arange(k)
    return np.exp2(a[idx // 512, idx % 128 // 32])


BF16 = ml_dtypes.bfloat16


def bf(x):
    return np.asarray(x, np.float32).astype(BF16)


def f64(x):
    return np.asarray(x).astype(np.float64)


B, S, HID, NH, DH, CHUNK = 1, 1024, 8192, 4, 128, 512
W = NH * DH
NC = S // CHUNK


def chunks(x):
    return x.reshape(B, S, NH, DH).transpose(0, 2, 1, 3).reshape(B, NH, NC, CHUNK, DH)


def with_prev(own, prev, op):
    return np.concatenate([own[:, :, :1], op(own[:, :, 1:], prev)], axis=2)


def setup_inputs():
    s = mx_kscale(HID)
    return {"q": bf(np.random.standard_normal((B, S, W)) * np.sqrt(2.0)),
            "k_scaled": bf(np.random.standard_normal((B, S, W)) * np.sqrt(2.0 / DH)),
            "hidden_states": bf(np.random.standard_normal((B, S, HID)) * s),
            "Wv": bf(np.random.standard_normal((HID, W)) / np.sqrt(HID) / s[:, None])}


def reference(q, k_scaled, hidden_states, Wv):
    q5, k5 = chunks(f64(q)), chunks(f64(k_scaled))
    v = mxq(f64(hidden_states), 2, "e4m3") @ mxq(f64(Wv), 0, "e4m3")
    vq = mxq(chunks(v), 3, "e4m3")
    pos = np.arange(CHUNK)
    later = np.where(pos[:, None] < pos[None, :], 1e9, 0.0)
    d_own = q5 @ k5.transpose(0, 1, 2, 4, 3) - later
    d_prev = q5[:, :, 1:] @ k5[:, :, :-1].transpose(0, 1, 2, 4, 3)
    m = with_prev(d_own.max(-1, keepdims=True), d_prev.max(-1, keepdims=True), np.maximum)
    e_own = np.exp(d_own - m)
    e_prev = np.exp(d_prev - m[:, :, 1:])
    den = with_prev(e_own.sum(-1, keepdims=True), e_prev.sum(-1, keepdims=True), np.add)
    num = with_prev(mxq(e_own, 4, "e4m3") @ vq, mxq(e_prev, 4, "e4m3") @ vq[:, :, :-1], np.add)
    res = num / den
    return res.reshape(B, NH, S, DH).transpose(0, 2, 1, 3).reshape(B, S, W)

@@ -1,0 +1,311 @@
+from contextlib import ExitStack
+
+import concourse.mybir as mybir
+from concourse.masks import make_identity
+
+BF16 = mybir.dt.bfloat16
+F32 = mybir.dt.float32
+U32 = mybir.dt.uint32
+U8 = mybir.dt.uint8
+FP8X4 = mybir.dt.float8_e4m3fn_x4
+ALU = mybir.AluOpType
+ACT = mybir.ActivationFunctionType
+
+P = 128
+PACK = 4
+K_PASS = P * PACK
+S = 1024
+HID = 8192
+NH = 4
+DH = 128
+W = NH * DH
+CHUNK = 512
+TILES = CHUNK // P
+PASSES = HID // K_PASS
+WORDS = K_PASS // 2
+MASKED = -1.0e9
+WV_VECTOR_COLS = 352
+
+FLOPS = 2 * S * HID * W + 2 * 2 * NH * 3 * CHUNK * CHUNK * DH
+
+
+def tile_localselfattention_pa_k_kernel(tc, q, k_scaled, hidden_states, Wv, out):
+    nc = tc.nc
+    q_rows = q.flatten_outer_dims()
+    k_rows = k_scaled.flatten_outer_dims()
+    x_rows = hidden_states.flatten_outer_dims()
+    out_rows = out.flatten_outer_dims()
+
+    with ExitStack() as ctx:
+        keep = ctx.enter_context(tc.tile_pool(name="keep", bufs=1))
+        stream = ctx.enter_context(tc.tile_pool(name="stream", bufs=2))
+        psum = ctx.enter_context(tc.psum_pool(name="psum", bufs=1))
+
+        ident_bf = keep.tile([P, P], BF16)
+        make_identity(nc, ident_bf[:])
+        ident_f32 = keep.tile([P, P], F32)
+        make_identity(nc, ident_f32[:])
+        later_f32 = keep.tile([P, P], F32)
+        nc.gpsimd.memset(later_f32[:], 0.0)
+        nc.gpsimd.affine_select(
+            out=later_f32[:],
+            in_=later_f32[:],
+            compare_op=ALU.is_ge,
+            fill=MASKED,
+            base=0,
+            pattern=[[-1, P]],
+            channel_multiplier=1,
+        )
+        later = keep.tile([P, P], BF16)
+        nc.vector.tensor_copy(out=later[:], in_=later_f32[:])
+
+        q_flipped = keep.tile([P, NH, S], BF16)
+        k_flipped = keep.tile([P, NH, S], BF16)
+        wv_codes = keep.tile([P, PASSES, W], U32, align_bytes=64)
+        wv_scales = keep.tile([P, PASSES, W], U8, align_bytes=64)
+        v_codes = keep.tile([P, 2, W], U32, align_bytes=64)
+        v_scales = keep.tile([P, 2, W], U8, align_bytes=64)
+        e_codes = keep.tile([P, 3 * TILES, W], U32, align_bytes=64)
+        e_scales = keep.tile([P, 3 * TILES, W], U8, align_bytes=64)
+        den = keep.tile([P, 2 * TILES * NH], F32)
+        own_grouped = []
+        for i in range(TILES):
+            grouped = keep.tile([P, NH, P, PACK], BF16, name="own_grouped%d" % i, align_bytes=64)
+            if i < TILES - 1:
+                nc.vector.memset(grouped[:], 0.0)
+            own_grouped.append(grouped)
+
+        def flip_heads(rows, flipped_all, n):
+            raw = stream.tile([P, TILES, W], BF16, tag="qk_raw")
+            nc.sync.dma_start(out=raw[:], in_=rows[n * CHUNK : (n + 1) * CHUNK, :].rearrange("(t p) w -> p t w", p=P))
+            for t in range(TILES):
+                flipped = psum.tile([P, NH, P], BF16, tag="e_flip")
+                for h in range(NH):
+                    nc.tensor.transpose(flipped[:, h, :], raw[:, t, h * DH : (h + 1) * DH], ident_bf[:])
+                first = n * CHUNK + t * P
+                nc.scalar.copy(out=flipped_all[:, :, first : first + P], in_=flipped[:])
+
+        def load_wv(a):
+            w_raw = stream.tile([P, 2 * PACK, W], BF16, tag="w_raw")
+            rows = Wv[a * 2 * K_PASS : (a + 1) * 2 * K_PASS, :]
+            nc.sync.dma_start(
+                out=w_raw[:].rearrange("p (s e) c -> p s (e c)", e=2),
+                in_=rows.rearrange("(s p e) c -> p s (e c)", p=P, e=2),
+            )
+            return w_raw
+
+        def quantise_wv(w_pass, g):
+            w_grouped = stream.tile([P, W, PACK], BF16, tag="w_grouped", align_bytes=64)
+            cut = WV_VECTOR_COLS
+            nc.vector.tensor_copy(
+                out=w_grouped[:, :cut, :].rearrange("p (c i) t -> p c t i", i=4),
+                in_=w_pass[:, :, :cut].rearrange("p t (c i) -> p c t i", i=4),
+            )
+            nc.scalar.copy(
+                out=w_grouped[:, cut:, :].rearrange("p (c i) t -> p c t i", i=4),
+                in_=w_pass[:, :, cut:].rearrange("p t (c i) -> p c t i", i=4),
+            )
+            nc.vector.quantize_mx(
+                out=wv_codes[:, g, :].bitcast(FP8X4),
+                scales=wv_scales[:, g, :],
+                in_=w_grouped[:].rearrange("p c t -> p (c t)"),
+            )
+
+        def flip_and_quantise(blocks, second_engine):
+            x_grouped = stream.tile([P, 4 * P * PACK], BF16, tag="x_grouped", bufs=3, align_bytes=64)
+            grouped_words = x_grouped[:].bitcast(F32).rearrange("p (r q u) -> p r q u", r=4, u=2)
+            for half in range(2):
+                flipped = psum.tile([P, 2, 2, P], F32, tag="x_flip", bufs=2)
+                for r in range(2):
+                    for u in range(2):
+                        nc.tensor.transpose(flipped[:, r, u, :], blocks[2 * half + r][:, u * P : (u + 1) * P], ident_f32[:])
+                dst = grouped_words[:, 2 * half : 2 * half + 2, :, :]
+                src = flipped[:].rearrange("p r u q -> p r q u")
+                if half == 0:
+                    nc.scalar.copy(out=dst, in_=src)
+                else:
+                    second_engine(out=dst, in_=src)
+            x_codes = stream.tile([P, 4 * P], U32, tag="x_codes", bufs=3, align_bytes=64)
+            x_scales = stream.tile([P, 4 * P], U8, tag="x_scales", bufs=3, align_bytes=64)
+            nc.vector.quantize_mx(out=x_codes[:].bitcast(FP8X4), scales=x_scales[:], in_=x_grouped[:])
+            return x_codes, x_scales
+
+        def project(acc, x_codes, x_scales, r, g):
+            cols = slice(r * P, (r + 1) * P)
+            nc.tensor.matmul_mx(
+                out=acc[:],
+                lhsT=x_codes[:, cols].bitcast(FP8X4),
+                lhsT_scale=x_scales[:, cols],
+                rhs=wv_codes[:, g, :].bitcast(FP8X4),
+                rhs_scale=wv_scales[:, g, :],
+                start=(g == 0),
+                stop=(g == PASSES - 1),
+            )
+
+        def quantise_v(v_rows, n):
+            v_grouped = stream.tile([P, W, PACK], BF16, tag="v_grouped", bufs=1, align_bytes=64)
+            nc.vector.tensor_copy(
+                out=v_grouped[:].rearrange("p (c i) t -> p c t i", i=4),
+                in_=v_rows[:].rearrange("p t (c i) -> p c t i", i=4),
+            )
+            nc.vector.quantize_mx(
+                out=v_codes[:, n, :].bitcast(FP8X4),
+                scales=v_scales[:, n, :],
+                in_=v_grouped[:].rearrange("p c t -> p (c t)"),
+            )
+
+        def softmax(j, h, prev_grouped, copy_engine):
+            n, i = divmod(j, TILES)
+            own = (i + 1) * P
+            queries = q_flipped[:, h, j * P : (j + 1) * P]
+            keys = k_flipped[:, h, n * CHUNK : n * CHUNK + own]
+            s_own = psum.tile([P, CHUNK], F32, tag="s_own")
+            if i > 0:
+                nc.tensor.matmul(s_own[:, : i * P], lhsT=queries, rhs=keys[:, : i * P], start=True, stop=True)
+            nc.tensor.matmul(s_own[:, i * P : own], lhsT=ident_bf[:], rhs=later[:], start=True, stop=False)
+            nc.tensor.matmul(s_own[:, i * P : own], lhsT=queries, rhs=keys[:, i * P : own], start=False, stop=True)
+            scores = stream.tile([P, 2 * CHUNK], F32, tag="scores")
+            tops = stream.tile([P, 2], F32, tag="tops")
+            neg_top = stream.tile([P, 1], F32, tag="neg_top")
+            nc.vector.tensor_scalar(
+                out=scores[:, CHUNK : CHUNK + own],
+                in0=s_own[:, :own],
+                scalar1=1.0,
+                scalar2=None,
+                op0=ALU.mult,
+                op1=ALU.max,
+                accum_out=tops[:, 0:1],
+            )
+            if n == 0:
+                first = CHUNK
+                nc.vector.tensor_scalar(out=neg_top[:], in0=tops[:, 0:1], scalar1=-1.0, scalar2=None, op0=ALU.mult)
+            else:
+                first = 0
+                s_prev = psum.tile([P, CHUNK], F32, tag="bank2")
+                nc.tensor.matmul(
+                    s_prev[:], lhsT=queries, rhs=k_flipped[:, h, (n - 1) * CHUNK : n * CHUNK], start=True, stop=True
+                )
+                nc.vector.tensor_scalar(
+                    out=scores[:, :CHUNK],
+                    in0=s_prev[:],
+                    scalar1=1.0,
+                    scalar2=None,
+                    op0=ALU.mult,
+                    op1=ALU.max,
+                    accum_out=tops[:, 1:2],
+                )
+                nc.vector.tensor_scalar(
+                    out=neg_top[:], in0=tops[:, 0:1], scalar1=tops[:, 1:2], scalar2=-1.0, op0=ALU.max, op1=ALU.mult
+                )
+            e = stream.tile([P, 2 * CHUNK], BF16, tag="e")
+            nc.scalar.activation(
+                out=e[:, first : CHUNK + own],
+                in_=scores[:, first : CHUNK + own],
+                func=ACT.Exp,
+                bias=neg_top[:],
+                scale=1.0,
+                accum_out=den[:, j * NH + h : j * NH + h + 1],
+            )
+            e_flip = psum.tile([P, 2 * TILES, P], BF16, tag="e_flip")
+            for b in range(first // P, (CHUNK + own) // P):
+                nc.tensor.transpose(e_flip[:, b, :], e[:, b * P : (b + 1) * P], ident_bf[:])
+            copy_engine(
+                out=own_grouped[i][:, h, :, : i + 1],
+                in_=e_flip[:, TILES : TILES + i + 1, :].rearrange("p t q -> p q t"),
+            )
+            if n > 0:
+                copy_engine(out=prev_grouped[:, h, :, :], in_=e_flip[:, :TILES, :].rearrange("p t q -> p q t"))
+
+        def quantise_e(grouped, slot):
+            nc.vector.quantize_mx(
+                out=e_codes[:, slot, :].bitcast(FP8X4),
+                scales=e_scales[:, slot, :],
+                in_=grouped[:].rearrange("p h q t -> p (h q t)"),
+            )
+
+        def attend(j, bank):
+            n, i = divmod(j, TILES)
+            o = psum.tile([P, W], F32, tag="bank%d" % bank)
+            for h in range(NH):
+                cols = slice(h * DH, (h + 1) * DH)
+                nc.tensor.matmul_mx(
+                    out=o[:, cols],
+                    lhsT=e_codes[:, j, cols].bitcast(FP8X4),
+                    lhsT_scale=e_scales[:, j, cols],
+                    rhs=v_codes[:, n, cols].bitcast(FP8X4),
+                    rhs_scale=v_scales[:, n, cols],
+                    start=True,
+                    stop=(n == 0),
+                )
+                if n > 0:
+                    nc.tensor.matmul_mx(
+                        out=o[:, cols],
+                        lhsT=e_codes[:, 2 * TILES + i, cols].bitcast(FP8X4),
+                        lhsT_scale=e_scales[:, 2 * TILES + i, cols],
+                        rhs=v_codes[:, n - 1, cols].bitcast(FP8X4),
+                        rhs_scale=v_scales[:, n - 1, cols],
+                        start=False,
+                        stop=True,
+                    )
+            recip = stream.tile([P, NH], F32, tag="recip")
+            nc.vector.reciprocal(out=recip[:], in_=den[:, j * NH : (j + 1) * NH])
+            o_sb = stream.tile([P, NH, DH], F32, tag="o_sb", bufs=3)
+            nc.vector.tensor_tensor(
+                out=o_sb[:],
+                in0=o[:].rearrange("p (h d) -> p h d", h=NH),
+                in1=recip[:].unsqueeze(2).to_broadcast([P, NH, DH]),
+                op=ALU.mult,
+            )
+            nc.sync.dma_start(out=out_rows[j * P : (j + 1) * P, :], in_=o_sb[:].rearrange("p h d -> p (h d)"))
+
+        flip_heads(q_rows, q_flipped, 0)
+        flip_heads(k_rows, k_flipped, 0)
+        accs = [psum.tile([P, W], F32, tag="bank%d" % t, name="acc%d" % t) for t in range(TILES)]
+        for a in range(PASSES // 2):
+            x_raw = stream.tile([P, TILES * 2 * K_PASS], BF16, tag="x_raw", bufs=3)
+            nc.sync.dma_start(
+                out=x_raw[:].rearrange("p (t k) -> p t k", t=TILES),
+                in_=x_rows[0:CHUNK, a * 2 * K_PASS : (a + 1) * 2 * K_PASS].rearrange("(t p) k -> p t k", p=P),
+            )
+            x_words = x_raw[:].bitcast(F32).rearrange("p (t g w) -> p t g w", t=TILES, g=2)
+            w_raw = load_wv(a)
+            for local in range(2):
+                g = 2 * a + local
+                quantise_wv(w_raw[:, local * PACK : (local + 1) * PACK, :], g)
+                x_codes, x_scales = flip_and_quantise([x_words[:, t, local, :] for t in range(TILES)], nc.scalar.copy)
+                for t in range(TILES):
+                    project(accs[t], x_codes, x_scales, t, g)
+                j, h = divmod(g, NH)
+                softmax(j, h, None, nc.scalar.copy)
+                if h == NH - 1:
+                    quantise_e(own_grouped[j], j)
+        v_rows = stream.tile([P, TILES, W], BF16, tag="v_rows")
+        for t in range(TILES):
+            nc.scalar.copy(out=v_rows[:, t, :], in_=accs[t][:])
+        quantise_v(v_rows, 0)
+
+        flip_heads(q_rows, q_flipped, 1)
+        flip_heads(k_rows, k_flipped, 1)
+        v_rows = stream.tile([P, TILES, W], BF16, tag="v_rows")
+        for j in range(TILES, 2 * TILES):
+            acc = psum.tile([P, W], F32, tag="bank%d" % (j % 2))
+            prev_grouped = stream.tile([P, NH, P, PACK], BF16, tag="prev_grouped", align_bytes=64)
+            for b in range(2):
+                x_raw = stream.tile([P, TILES * 2 * K_PASS], BF16, tag="x_raw", bufs=3)
+                nc.sync.dma_start(out=x_raw[:], in_=x_rows[j * P : (j + 1) * P, b * 8 * K_PASS : (b + 1) * 8 * K_PASS])
+                x_words = x_raw[:].bitcast(F32).rearrange("p (g w) -> p g w", w=WORDS)
+                for s in range(2):
+                    h = 2 * b + s
+                    x_codes, x_scales = flip_and_quantise(
+                        [x_words[:, 4 * s + r, :] for r in range(4)], nc.vector.tensor_copy
+                    )
+                    for r in range(4):
+                        project(acc, x_codes, x_scales, r, 4 * h + r)
+                    softmax(j, h, prev_grouped, nc.vector.tensor_copy if h % 2 == 0 else nc.scalar.copy)
+            quantise_e(own_grouped[j - TILES], j)
+            quantise_e(prev_grouped, TILES + j)
+            nc.scalar.copy(out=v_rows[:, j - TILES, :], in_=acc[:])
+            attend(j - TILES, 3)
+        quantise_v(v_rows, 1)
+        for j in range(TILES, 2 * TILES):
+            attend(j, j % TILES)

@@ -23,8 +23,10 @@ CHUNK = 512
 TILES = CHUNK // P
 PASSES = HID // K_PASS
 WORDS = K_PASS // 2
+STEPS = 2 * PASSES
+LOAD_COLS = 2 * TILES * K_PASS
 MASKED = -1.0e9
-WV_VECTOR_COLS = 352
+WV_VECTOR_COLS = 368
 
 FLOPS = 2 * S * HID * W + 2 * 2 * NH * 3 * CHUNK * CHUNK * DH
 
@@ -37,6 +39,7 @@ def tile_localselfattention_pa_k_kernel(tc, q, k_scaled, hidden_states, Wv, out)
     out_rows = out.flatten_outer_dims()
 
     with ExitStack() as ctx:
+        ctx.enter_context(tc.manual_schedule())
         keep = ctx.enter_context(tc.tile_pool(name="keep", bufs=1))
         stream = ctx.enter_context(tc.tile_pool(name="stream", bufs=2))
         psum = ctx.enter_context(tc.psum_pool(name="psum", bufs=1))
@@ -75,78 +78,143 @@ def tile_localselfattention_pa_k_kernel(tc, q, k_scaled, hidden_states, Wv, out)
                 nc.vector.memset(grouped[:], 0.0)
             own_grouped.append(grouped)
 
-        def flip_heads(rows, flipped_all, n):
-            raw = stream.tile([P, TILES, W], BF16, tag="qk_raw")
-            nc.sync.dma_start(out=raw[:], in_=rows[n * CHUNK : (n + 1) * CHUNK, :].rearrange("(t p) w -> p t w", p=P))
-            for t in range(TILES):
-                flipped = psum.tile([P, NH, P], BF16, tag="e_flip")
+        x_blocks = {}
+        w_passes = {}
+        x_grouped_of = {}
+        w_grouped_of = {}
+        x_quantised = {}
+        accs = {}
+        scores_psum = {}
+        scores_of = {}
+        e_of = {}
+        e_flip_of = {}
+        prev_grouped_of = {}
+        v_rows_of = {}
+
+        def load_whole(rows):
+            raw = stream.tile([P, LOAD_COLS], BF16, tag="x_raw", bufs=4)
+            nc.sync.dma_start(
+                out=raw[:].rearrange("p (t w) -> p t w", w=W), in_=rows.rearrange("(t p) w -> p t w", p=P)
+            )
+            return raw[:].rearrange("p (t w) -> p t w", w=W)
+
+        def flip_heads(raw, flipped_all):
+            for t in range(2 * TILES):
+                flipped = psum.tile([P, NH, P], BF16, tag="bank%d" % (t % TILES))
                 for h in range(NH):
                     nc.tensor.transpose(flipped[:, h, :], raw[:, t, h * DH : (h + 1) * DH], ident_bf[:])
-                first = n * CHUNK + t * P
-                nc.scalar.copy(out=flipped_all[:, :, first : first + P], in_=flipped[:])
+                dst = flipped_all[:, :, t * P : (t + 1) * P]
+                if t % 2 == 0:
+                    nc.scalar.copy(out=dst, in_=flipped[:])
+                else:
+                    nc.vector.tensor_copy(out=dst, in_=flipped[:])
+
+        def load_hidden(a):
+            x_raw = stream.tile([P, LOAD_COLS], BF16, tag="x_raw", bufs=4)
+            if 2 * a < PASSES:
+                cols = slice(a * 2 * K_PASS, (a + 1) * 2 * K_PASS)
+                nc.sync.dma_start(
+                    out=x_raw[:].rearrange("p (t k) -> p t k", t=TILES),
+                    in_=x_rows[0:CHUNK, cols].rearrange("(t p) k -> p t k", p=P),
+                )
+                words = x_raw[:].bitcast(F32).rearrange("p (t g w) -> p t g w", t=TILES, g=2)
+                for local in range(2):
+                    x_blocks[2 * a + local] = [words[:, t, local, :] for t in range(TILES)]
+            else:
+                j, b = divmod(a, 2)
+                nc.sync.dma_start(out=x_raw[:], in_=x_rows[j * P : (j + 1) * P, b * LOAD_COLS : (b + 1) * LOAD_COLS])
+                words = x_raw[:].bitcast(F32).rearrange("p (g w) -> p g w", w=WORDS)
+                for local in range(2):
+                    x_blocks[2 * a + local] = [words[:, 4 * local + r, :] for r in range(4)]
 
         def load_wv(a):
-            w_raw = stream.tile([P, 2 * PACK, W], BF16, tag="w_raw")
+            w_raw = stream.tile([P, 2 * PACK, W], BF16, tag="w_raw", bufs=3)
             rows = Wv[a * 2 * K_PASS : (a + 1) * 2 * K_PASS, :]
             nc.sync.dma_start(
                 out=w_raw[:].rearrange("p (s e) c -> p s (e c)", e=2),
                 in_=rows.rearrange("(s p e) c -> p s (e c)", p=P, e=2),
             )
-            return w_raw
+            for local in range(2):
+                w_passes[2 * a + local] = w_raw[:, local * PACK : (local + 1) * PACK, :]
 
-        def quantise_wv(w_pass, g):
+        def regroup_wv(g):
             w_grouped = stream.tile([P, W, PACK], BF16, tag="w_grouped", align_bytes=64)
+            w_grouped_of[g] = w_grouped
             cut = WV_VECTOR_COLS
             nc.vector.tensor_copy(
                 out=w_grouped[:, :cut, :].rearrange("p (c i) t -> p c t i", i=4),
-                in_=w_pass[:, :, :cut].rearrange("p t (c i) -> p c t i", i=4),
+                in_=w_passes[g][:, :, :cut].rearrange("p t (c i) -> p c t i", i=4),
             )
             nc.scalar.copy(
                 out=w_grouped[:, cut:, :].rearrange("p (c i) t -> p c t i", i=4),
-                in_=w_pass[:, :, cut:].rearrange("p t (c i) -> p c t i", i=4),
+                in_=w_passes[g][:, :, cut:].rearrange("p t (c i) -> p c t i", i=4),
             )
+
+        def quantise_wv(g):
             nc.vector.quantize_mx(
                 out=wv_codes[:, g, :].bitcast(FP8X4),
                 scales=wv_scales[:, g, :],
-                in_=w_grouped[:].rearrange("p c t -> p (c t)"),
+                in_=w_grouped_of[g][:].rearrange("p c t -> p (c t)"),
             )
 
-        def flip_and_quantise(blocks, second_engine):
-            x_grouped = stream.tile([P, 4 * P * PACK], BF16, tag="x_grouped", bufs=3, align_bytes=64)
+        def flip_hidden(s):
+            x_grouped = stream.tile([P, 4 * P * PACK], BF16, tag="x_grouped", align_bytes=64)
+            x_grouped_of[s] = x_grouped
             grouped_words = x_grouped[:].bitcast(F32).rearrange("p (r q u) -> p r q u", r=4, u=2)
             for half in range(2):
                 flipped = psum.tile([P, 2, 2, P], F32, tag="x_flip", bufs=2)
                 for r in range(2):
                     for u in range(2):
-                        nc.tensor.transpose(flipped[:, r, u, :], blocks[2 * half + r][:, u * P : (u + 1) * P], ident_f32[:])
+                        nc.tensor.transpose(
+                            flipped[:, r, u, :], x_blocks[s][2 * half + r][:, u * P : (u + 1) * P], ident_f32[:]
+                        )
                 dst = grouped_words[:, 2 * half : 2 * half + 2, :, :]
                 src = flipped[:].rearrange("p r u q -> p r q u")
-                if half == 0:
+                if half == 0 or s < PASSES:
                     nc.scalar.copy(out=dst, in_=src)
                 else:
-                    second_engine(out=dst, in_=src)
+                    nc.vector.tensor_copy(out=dst, in_=src)
+
+        def quantise_hidden(s):
             x_codes = stream.tile([P, 4 * P], U32, tag="x_codes", bufs=3, align_bytes=64)
             x_scales = stream.tile([P, 4 * P], U8, tag="x_scales", bufs=3, align_bytes=64)
-            nc.vector.quantize_mx(out=x_codes[:].bitcast(FP8X4), scales=x_scales[:], in_=x_grouped[:])
-            return x_codes, x_scales
+            nc.vector.quantize_mx(out=x_codes[:].bitcast(FP8X4), scales=x_scales[:], in_=x_grouped_of[s][:])
+            x_quantised[s] = (x_codes, x_scales)
 
-        def project(acc, x_codes, x_scales, r, g):
-            cols = slice(r * P, (r + 1) * P)
-            nc.tensor.matmul_mx(
-                out=acc[:],
-                lhsT=x_codes[:, cols].bitcast(FP8X4),
-                lhsT_scale=x_scales[:, cols],
-                rhs=wv_codes[:, g, :].bitcast(FP8X4),
-                rhs_scale=wv_scales[:, g, :],
-                start=(g == 0),
-                stop=(g == PASSES - 1),
-            )
+        def project(s):
+            x_codes, x_scales = x_quantised[s]
+            for r in range(4):
+                if s < PASSES:
+                    tile_of_positions, g = r, s
+                else:
+                    tile_of_positions, g = s // 4, 4 * (s % 4) + r
+                if g == 0:
+                    accs[tile_of_positions] = psum.tile(
+                        [P, W],
+                        F32,
+                        tag="bank%d" % (r if s < PASSES else tile_of_positions % 2),
+                        name="acc%d" % tile_of_positions,
+                    )
+                cols = slice(r * P, (r + 1) * P)
+                nc.tensor.matmul_mx(
+                    out=accs[tile_of_positions][:],
+                    lhsT=x_codes[:, cols].bitcast(FP8X4),
+                    lhsT_scale=x_scales[:, cols],
+                    rhs=wv_codes[:, g, :].bitcast(FP8X4),
+                    rhs_scale=wv_scales[:, g, :],
+                    start=(g == 0),
+                    stop=(g == PASSES - 1),
+                )
 
-        def quantise_v(v_rows, n):
+        def round_v(tile_of_positions, copy):
+            n, t = divmod(tile_of_positions, TILES)
+            copy(out=v_rows_of[n][:, t, :], in_=accs[tile_of_positions][:])
+
+        def quantise_v(n):
             v_grouped = stream.tile([P, W, PACK], BF16, tag="v_grouped", bufs=1, align_bytes=64)
             nc.vector.tensor_copy(
                 out=v_grouped[:].rearrange("p (c i) t -> p c t i", i=4),
-                in_=v_rows[:].rearrange("p t (c i) -> p c t i", i=4),
+                in_=v_rows_of[n][:].rearrange("p t (c i) -> p c t i", i=4),
             )
             nc.vector.quantize_mx(
                 out=v_codes[:, n, :].bitcast(FP8X4),
@@ -154,7 +222,8 @@ def tile_localselfattention_pa_k_kernel(tc, q, k_scaled, hidden_states, Wv, out)
                 in_=v_grouped[:].rearrange("p c t -> p (c t)"),
             )
 
-        def softmax(j, h, prev_grouped, copy_engine):
+        def score(s):
+            j, h = divmod(s, NH)
             n, i = divmod(j, TILES)
             own = (i + 1) * P
             queries = q_flipped[:, h, j * P : (j + 1) * P]
@@ -164,66 +233,94 @@ def tile_localselfattention_pa_k_kernel(tc, q, k_scaled, hidden_states, Wv, out)
                 nc.tensor.matmul(s_own[:, : i * P], lhsT=queries, rhs=keys[:, : i * P], start=True, stop=True)
             nc.tensor.matmul(s_own[:, i * P : own], lhsT=ident_bf[:], rhs=later[:], start=True, stop=False)
             nc.tensor.matmul(s_own[:, i * P : own], lhsT=queries, rhs=keys[:, i * P : own], start=False, stop=True)
-            scores = stream.tile([P, 2 * CHUNK], F32, tag="scores")
-            tops = stream.tile([P, 2], F32, tag="tops")
-            neg_top = stream.tile([P, 1], F32, tag="neg_top")
-            nc.vector.tensor_scalar(
-                out=scores[:, CHUNK : CHUNK + own],
-                in0=s_own[:, :own],
-                scalar1=1.0,
-                scalar2=None,
-                op0=ALU.mult,
-                op1=ALU.max,
-                accum_out=tops[:, 0:1],
-            )
-            if n == 0:
-                first = CHUNK
-                nc.vector.tensor_scalar(out=neg_top[:], in0=tops[:, 0:1], scalar1=-1.0, scalar2=None, op0=ALU.mult)
-            else:
-                first = 0
+            s_prev = None
+            if n > 0:
                 s_prev = psum.tile([P, CHUNK], F32, tag="bank2")
                 nc.tensor.matmul(
                     s_prev[:], lhsT=queries, rhs=k_flipped[:, h, (n - 1) * CHUNK : n * CHUNK], start=True, stop=True
                 )
+            scores_psum[s] = (s_own, s_prev)
+
+        def top(s):
+            n, i = divmod(s // NH, TILES)
+            own = (i + 1) * P
+            s_own, s_prev = scores_psum[s]
+            minus_scores = stream.tile([P, 2 * CHUNK], F32, tag="minus_scores")
+            minus_top = stream.tile([P, 2], F32, tag="minus_top")
+            nc.vector.tensor_scalar(
+                out=minus_scores[:, CHUNK : CHUNK + own],
+                in0=s_own[:, :own],
+                scalar1=-1.0,
+                scalar2=None,
+                op0=ALU.mult,
+                op1=ALU.min,
+                accum_out=minus_top[:, 0:1],
+            )
+            if n > 0:
                 nc.vector.tensor_scalar(
-                    out=scores[:, :CHUNK],
+                    out=minus_scores[:, :CHUNK],
                     in0=s_prev[:],
-                    scalar1=1.0,
-                    scalar2=None,
+                    scalar1=-1.0,
+                    scalar2=minus_top[:, 0:1],
                     op0=ALU.mult,
-                    op1=ALU.max,
-                    accum_out=tops[:, 1:2],
+                    op1=ALU.min,
+                    accum_out=minus_top[:, 1:2],
                 )
-                nc.vector.tensor_scalar(
-                    out=neg_top[:], in0=tops[:, 0:1], scalar1=tops[:, 1:2], scalar2=-1.0, op0=ALU.max, op1=ALU.mult
-                )
+            scores_of[s] = (minus_scores, minus_top[:, n : n + 1])
+
+        def exponential(s):
+            n, i = divmod(s // NH, TILES)
+            first = CHUNK * (1 - n)
+            last = CHUNK + (i + 1) * P
+            minus_scores, minus_top = scores_of[s]
             e = stream.tile([P, 2 * CHUNK], BF16, tag="e")
             nc.scalar.activation(
-                out=e[:, first : CHUNK + own],
-                in_=scores[:, first : CHUNK + own],
+                out=e[:, first:last],
+                in_=minus_scores[:, first:last],
                 func=ACT.Exp,
-                bias=neg_top[:],
-                scale=1.0,
-                accum_out=den[:, j * NH + h : j * NH + h + 1],
+                bias=minus_top,
+                scale=-1.0,
+                accum_out=den[:, s : s + 1],
             )
+            e_of[s] = e
+
+        def flip_e(s):
+            n, i = divmod(s // NH, TILES)
             e_flip = psum.tile([P, 2 * TILES, P], BF16, tag="e_flip")
-            for b in range(first // P, (CHUNK + own) // P):
-                nc.tensor.transpose(e_flip[:, b, :], e[:, b * P : (b + 1) * P], ident_bf[:])
-            copy_engine(
+            for b in range(TILES * (1 - n), TILES + i + 1):
+                nc.tensor.transpose(e_flip[:, b, :], e_of[s][:, b * P : (b + 1) * P], ident_bf[:])
+            e_flip_of[s] = e_flip
+
+        def regroup_e(s):
+            j, h = divmod(s, NH)
+            n, i = divmod(j, TILES)
+            e_flip = e_flip_of[s]
+            nc.scalar.copy(
                 out=own_grouped[i][:, h, :, : i + 1],
                 in_=e_flip[:, TILES : TILES + i + 1, :].rearrange("p t q -> p q t"),
             )
             if n > 0:
-                copy_engine(out=prev_grouped[:, h, :, :], in_=e_flip[:, :TILES, :].rearrange("p t q -> p q t"))
+                if h == 0:
+                    prev_grouped_of[j] = stream.tile(
+                        [P, NH, P, PACK], BF16, tag="prev_grouped", name="prev_grouped", align_bytes=64
+                    )
+                nc.scalar.copy(out=prev_grouped_of[j][:, h, :, :], in_=e_flip[:, :TILES, :].rearrange("p t q -> p q t"))
 
-        def quantise_e(grouped, slot):
+        def quantise_e(j):
+            n, i = divmod(j, TILES)
             nc.vector.quantize_mx(
-                out=e_codes[:, slot, :].bitcast(FP8X4),
-                scales=e_scales[:, slot, :],
-                in_=grouped[:].rearrange("p h q t -> p (h q t)"),
+                out=e_codes[:, j, :].bitcast(FP8X4),
+                scales=e_scales[:, j, :],
+                in_=own_grouped[i][:].rearrange("p h q t -> p (h q t)"),
             )
+            if n > 0:
+                nc.vector.quantize_mx(
+                    out=e_codes[:, 2 * TILES + i, :].bitcast(FP8X4),
+                    scales=e_scales[:, 2 * TILES + i, :],
+                    in_=prev_grouped_of[j][:].rearrange("p h q t -> p (h q t)"),
+                )
 
-        def attend(j, bank):
+        def attend(j, bank, on_vector):
             n, i = divmod(j, TILES)
             o = psum.tile([P, W], F32, tag="bank%d" % bank)
             for h in range(NH):
@@ -249,63 +346,75 @@ def tile_localselfattention_pa_k_kernel(tc, q, k_scaled, hidden_states, Wv, out)
                     )
             recip = stream.tile([P, NH], F32, tag="recip")
             nc.vector.reciprocal(out=recip[:], in_=den[:, j * NH : (j + 1) * NH])
-            o_sb = stream.tile([P, NH, DH], F32, tag="o_sb", bufs=3)
-            nc.vector.tensor_tensor(
-                out=o_sb[:],
-                in0=o[:].rearrange("p (h d) -> p h d", h=NH),
-                in1=recip[:].unsqueeze(2).to_broadcast([P, NH, DH]),
-                op=ALU.mult,
-            )
+            o_sb = stream.tile([P, NH, DH], F32, tag="o_sb")
+            if on_vector:
+                nc.vector.tensor_tensor(
+                    out=o_sb[:],
+                    in0=o[:].rearrange("p (h d) -> p h d", h=NH),
+                    in1=recip[:].unsqueeze(2).to_broadcast([P, NH, DH]),
+                    op=ALU.mult,
+                )
+            else:
+                for h in range(NH):
+                    nc.scalar.activation(
+                        out=o_sb[:, h, :], in_=o[:, h * DH : (h + 1) * DH], func=ACT.Copy, scale=recip[:, h : h + 1]
+                    )
             nc.sync.dma_start(out=out_rows[j * P : (j + 1) * P, :], in_=o_sb[:].rearrange("p h d -> p (h d)"))
 
-        flip_heads(q_rows, q_flipped, 0)
-        flip_heads(k_rows, k_flipped, 0)
-        accs = [psum.tile([P, W], F32, tag="bank%d" % t, name="acc%d" % t) for t in range(TILES)]
-        for a in range(PASSES // 2):
-            x_raw = stream.tile([P, TILES * 2 * K_PASS], BF16, tag="x_raw", bufs=3)
-            nc.sync.dma_start(
-                out=x_raw[:].rearrange("p (t k) -> p t k", t=TILES),
-                in_=x_rows[0:CHUNK, a * 2 * K_PASS : (a + 1) * 2 * K_PASS].rearrange("(t p) k -> p t k", p=P),
-            )
-            x_words = x_raw[:].bitcast(F32).rearrange("p (t g w) -> p t g w", t=TILES, g=2)
-            w_raw = load_wv(a)
-            for local in range(2):
-                g = 2 * a + local
-                quantise_wv(w_raw[:, local * PACK : (local + 1) * PACK, :], g)
-                x_codes, x_scales = flip_and_quantise([x_words[:, t, local, :] for t in range(TILES)], nc.scalar.copy)
-                for t in range(TILES):
-                    project(accs[t], x_codes, x_scales, t, g)
-                j, h = divmod(g, NH)
-                softmax(j, h, None, nc.scalar.copy)
-                if h == NH - 1:
-                    quantise_e(own_grouped[j], j)
-        v_rows = stream.tile([P, TILES, W], BF16, tag="v_rows")
-        for t in range(TILES):
-            nc.scalar.copy(out=v_rows[:, t, :], in_=accs[t][:])
-        quantise_v(v_rows, 0)
+        q_raw = load_whole(q_rows)
+        k_raw = load_whole(k_rows)
+        load_hidden(0)
+        load_wv(0)
+        load_hidden(1)
+        load_wv(1)
+        flip_heads(q_raw, q_flipped)
+        flip_heads(k_raw, k_flipped)
+        flip_hidden(0)
+        regroup_wv(0)
+        score(0)
+        quantise_wv(0)
+        quantise_hidden(0)
+        for n in range(2):
+            v_rows_of[n] = stream.tile([P, TILES, W], BF16, tag="v_rows", name="v_rows")
 
-        flip_heads(q_rows, q_flipped, 1)
-        flip_heads(k_rows, k_flipped, 1)
-        v_rows = stream.tile([P, TILES, W], BF16, tag="v_rows")
+        for s in range(STEPS):
+            top(s)
+            if s + 1 < STEPS:
+                flip_hidden(s + 1)
+            if s >= 1:
+                flip_e(s - 1)
+            if s + 1 < PASSES:
+                regroup_wv(s + 1)
+            exponential(s)
+            if s >= 1:
+                regroup_e(s - 1)
+            if s + 1 < STEPS:
+                quantise_hidden(s + 1)
+            if s + 1 < PASSES:
+                quantise_wv(s + 1)
+            if s >= NH and s % NH == 0:
+                quantise_e(s // NH - 1)
+            if s == PASSES:
+                quantise_v(0)
+            project(s)
+            if s == PASSES - 1:
+                round_v(2, nc.scalar.copy)
+                round_v(1, nc.vector.tensor_copy)
+                round_v(0, nc.scalar.copy)
+                round_v(3, nc.vector.tensor_copy)
+            if s >= PASSES and s % 4 == 3:
+                round_v(s // 4, nc.scalar.copy)
+                attend(s // 4 - TILES, 3, True)
+            if s + 1 < STEPS:
+                score(s + 1)
+            if s % 2 == 0 and s // 2 + 2 < STEPS // 2:
+                load_hidden(s // 2 + 2)
+                if s + 4 < PASSES:
+                    load_wv(s // 2 + 2)
+
+        flip_e(STEPS - 1)
+        regroup_e(STEPS - 1)
+        quantise_v(1)
+        quantise_e(2 * TILES - 1)
         for j in range(TILES, 2 * TILES):
-            acc = psum.tile([P, W], F32, tag="bank%d" % (j % 2))
-            prev_grouped = stream.tile([P, NH, P, PACK], BF16, tag="prev_grouped", align_bytes=64)
-            for b in range(2):
-                x_raw = stream.tile([P, TILES * 2 * K_PASS], BF16, tag="x_raw", bufs=3)
-                nc.sync.dma_start(out=x_raw[:], in_=x_rows[j * P : (j + 1) * P, b * 8 * K_PASS : (b + 1) * 8 * K_PASS])
-                x_words = x_raw[:].bitcast(F32).rearrange("p (g w) -> p g w", w=WORDS)
-                for s in range(2):
-                    h = 2 * b + s
-                    x_codes, x_scales = flip_and_quantise(
-                        [x_words[:, 4 * s + r, :] for r in range(4)], nc.vector.tensor_copy
-                    )
-                    for r in range(4):
-                        project(acc, x_codes, x_scales, r, 4 * h + r)
-                    softmax(j, h, prev_grouped, nc.vector.tensor_copy if h % 2 == 0 else nc.scalar.copy)
-            quantise_e(own_grouped[j - TILES], j)
-            quantise_e(prev_grouped, TILES + j)
-            nc.scalar.copy(out=v_rows[:, j - TILES, :], in_=acc[:])
-            attend(j - TILES, 3)
-        quantise_v(v_rows, 1)
-        for j in range(TILES, 2 * TILES):
-            attend(j, j % TILES)
+            attend(j, j % TILES, j % 2 == 0)

@@ -27,6 +27,7 @@ STEPS = 2 * PASSES
 LOAD_COLS = 2 * TILES * K_PASS
 MASKED = -1.0e9
 WV_VECTOR_COLS = 368
+QK_FLIP_STEP = 8
 
 FLOPS = 2 * S * HID * W + 2 * 2 * NH * 3 * CHUNK * CHUNK * DH
 
@@ -91,51 +92,48 @@ def tile_localselfattention_pa_k_kernel(tc, q, k_scaled, hidden_states, Wv, out)
         prev_grouped_of = {}
         v_rows_of = {}
 
-        def load_whole(rows):
+        def load_qk(n):
             raw = stream.tile([P, LOAD_COLS], BF16, tag="x_raw", bufs=4)
-            nc.sync.dma_start(
-                out=raw[:].rearrange("p (t w) -> p t w", w=W), in_=rows.rearrange("(t p) w -> p t w", p=P)
-            )
-            return raw[:].rearrange("p (t w) -> p t w", w=W)
-
-        def flip_heads(raw, flipped_all):
-            for t in range(2 * TILES):
-                flipped = psum.tile([P, NH, P], BF16, tag="bank%d" % (t % TILES))
-                for h in range(NH):
-                    nc.tensor.transpose(flipped[:, h, :], raw[:, t, h * DH : (h + 1) * DH], ident_bf[:])
-                dst = flipped_all[:, :, t * P : (t + 1) * P]
-                if t % 2 == 0:
-                    nc.scalar.copy(out=dst, in_=flipped[:])
-                else:
-                    nc.vector.tensor_copy(out=dst, in_=flipped[:])
-
-        def load_hidden(a):
-            x_raw = stream.tile([P, LOAD_COLS], BF16, tag="x_raw", bufs=4)
-            if 2 * a < PASSES:
-                cols = slice(a * 2 * K_PASS, (a + 1) * 2 * K_PASS)
+            qk_raw = raw[:].rearrange("p (o t w) -> p o t w", o=2, w=W)
+            for o, rows in enumerate((q_rows, k_rows)):
                 nc.sync.dma_start(
-                    out=x_raw[:].rearrange("p (t k) -> p t k", t=TILES),
-                    in_=x_rows[0:CHUNK, cols].rearrange("(t p) k -> p t k", p=P),
+                    out=qk_raw[:, o, :, :], in_=rows[n * CHUNK : (n + 1) * CHUNK, :].rearrange("(t p) w -> p t w", p=P)
                 )
-                words = x_raw[:].bitcast(F32).rearrange("p (t g w) -> p t g w", t=TILES, g=2)
-                for local in range(2):
-                    x_blocks[2 * a + local] = [words[:, t, local, :] for t in range(TILES)]
-            else:
-                j, b = divmod(a, 2)
-                nc.sync.dma_start(out=x_raw[:], in_=x_rows[j * P : (j + 1) * P, b * LOAD_COLS : (b + 1) * LOAD_COLS])
-                words = x_raw[:].bitcast(F32).rearrange("p (g w) -> p g w", w=WORDS)
-                for local in range(2):
-                    x_blocks[2 * a + local] = [words[:, 4 * local + r, :] for r in range(4)]
+            return qk_raw
 
-        def load_wv(a):
-            w_raw = stream.tile([P, 2 * PACK, W], BF16, tag="w_raw", bufs=3)
-            rows = Wv[a * 2 * K_PASS : (a + 1) * 2 * K_PASS, :]
+        def flip_qk(qk_raw, tile_of_positions, flipped, copy):
+            t = tile_of_positions % TILES
+            for o in range(2):
+                for h in range(NH):
+                    nc.tensor.transpose(flipped[:, o, h, :], qk_raw[:, o, t, h * DH : (h + 1) * DH], ident_bf[:])
+            positions = slice(tile_of_positions * P, (tile_of_positions + 1) * P)
+            copy(out=q_flipped[:, :, positions], in_=flipped[:, 0, :, :])
+            copy(out=k_flipped[:, :, positions], in_=flipped[:, 1, :, :])
+
+        def load_passes(g, count):
+            x_raw = stream.tile([P, LOAD_COLS], BF16, tag="x_raw", bufs=4)
+            used = x_raw[:, : TILES * count * K_PASS]
             nc.sync.dma_start(
-                out=w_raw[:].rearrange("p (s e) c -> p s (e c)", e=2),
-                in_=rows.rearrange("(s p e) c -> p s (e c)", p=P, e=2),
+                out=used.rearrange("p (t k) -> p t k", t=TILES),
+                in_=x_rows[0:CHUNK, g * K_PASS : (g + count) * K_PASS].rearrange("(t p) k -> p t k", p=P),
             )
+            words = used.bitcast(F32).rearrange("p (t g w) -> p t g w", t=TILES, w=WORDS)
+            w_raw = stream.tile([P, 2 * PACK, W], BF16, tag="w_raw", bufs=3)
+            nc.sync.dma_start(
+                out=w_raw[:, : count * PACK, :].rearrange("p (s e) c -> p s (e c)", e=2),
+                in_=Wv[g * K_PASS : (g + count) * K_PASS, :].rearrange("(s p e) c -> p s (e c)", p=P, e=2),
+            )
+            for local in range(count):
+                x_blocks[g + local] = [words[:, t, local, :] for t in range(TILES)]
+                w_passes[g + local] = w_raw[:, local * PACK : (local + 1) * PACK, :]
+
+        def load_half_tile(s):
+            x_raw = stream.tile([P, LOAD_COLS], BF16, tag="x_raw", bufs=4)
+            j, b = divmod(s // 2, 2)
+            nc.sync.dma_start(out=x_raw[:], in_=x_rows[j * P : (j + 1) * P, b * LOAD_COLS : (b + 1) * LOAD_COLS])
+            words = x_raw[:].bitcast(F32).rearrange("p (g w) -> p g w", w=WORDS)
             for local in range(2):
-                w_passes[2 * a + local] = w_raw[:, local * PACK : (local + 1) * PACK, :]
+                x_blocks[s + local] = [words[:, 4 * local + r, :] for r in range(4)]
 
         def regroup_wv(g):
             w_grouped = stream.tile([P, W, PACK], BF16, tag="w_grouped", align_bytes=64)
@@ -241,32 +239,37 @@ def tile_localselfattention_pa_k_kernel(tc, q, k_scaled, hidden_states, Wv, out)
                 )
             scores_psum[s] = (s_own, s_prev)
 
-        def top(s):
-            n, i = divmod(s // NH, TILES)
-            own = (i + 1) * P
-            s_own, s_prev = scores_psum[s]
+        def top_prev(s):
             minus_scores = stream.tile([P, 2 * CHUNK], F32, tag="minus_scores")
             minus_top = stream.tile([P, 2], F32, tag="minus_top")
+            scores_of[s] = (minus_scores, minus_top)
             nc.vector.tensor_scalar(
-                out=minus_scores[:, CHUNK : CHUNK + own],
-                in0=s_own[:, :own],
+                out=minus_scores[:, :CHUNK],
+                in0=scores_psum[s][1][:],
                 scalar1=-1.0,
                 scalar2=None,
                 op0=ALU.mult,
                 op1=ALU.min,
                 accum_out=minus_top[:, 0:1],
             )
-            if n > 0:
-                nc.vector.tensor_scalar(
-                    out=minus_scores[:, :CHUNK],
-                    in0=s_prev[:],
-                    scalar1=-1.0,
-                    scalar2=minus_top[:, 0:1],
-                    op0=ALU.mult,
-                    op1=ALU.min,
-                    accum_out=minus_top[:, 1:2],
-                )
-            scores_of[s] = (minus_scores, minus_top[:, n : n + 1])
+
+        def top_own(s):
+            n, i = divmod(s // NH, TILES)
+            own = (i + 1) * P
+            if n == 0:
+                minus_scores = stream.tile([P, 2 * CHUNK], F32, tag="minus_scores")
+                minus_top = stream.tile([P, 2], F32, tag="minus_top")
+                scores_of[s] = (minus_scores, minus_top)
+            minus_scores, minus_top = scores_of[s]
+            nc.vector.tensor_scalar(
+                out=minus_scores[:, CHUNK : CHUNK + own],
+                in0=scores_psum[s][0][:, :own],
+                scalar1=-1.0,
+                scalar2=(minus_top[:, 0:1] if n > 0 else None),
+                op0=ALU.mult,
+                op1=ALU.min,
+                accum_out=minus_top[:, 1:2],
+            )
 
         def exponential(s):
             n, i = divmod(s // NH, TILES)
@@ -278,7 +281,7 @@ def tile_localselfattention_pa_k_kernel(tc, q, k_scaled, hidden_states, Wv, out)
                 out=e[:, first:last],
                 in_=minus_scores[:, first:last],
                 func=ACT.Exp,
-                bias=minus_top,
+                bias=minus_top[:, 1:2],
                 scale=-1.0,
                 accum_out=den[:, s : s + 1],
             )
@@ -361,33 +364,37 @@ def tile_localselfattention_pa_k_kernel(tc, q, k_scaled, hidden_states, Wv, out)
                     )
             nc.sync.dma_start(out=out_rows[j * P : (j + 1) * P, :], in_=o_sb[:].rearrange("p h d -> p (h d)"))
 
-        q_raw = load_whole(q_rows)
-        k_raw = load_whole(k_rows)
-        load_hidden(0)
-        load_wv(0)
-        load_hidden(1)
-        load_wv(1)
-        flip_heads(q_raw, q_flipped)
-        flip_heads(k_raw, k_flipped)
+        qk_raw = load_qk(0)
+        load_passes(0, 1)
+        load_passes(1, 1)
+        load_passes(2, 2)
+        for t in range(TILES):
+            flipped = psum.tile([P, 2, NH, P], BF16, tag="bank%d" % t)
+            flip_qk(qk_raw, t, flipped, nc.scalar.copy if t % 2 == 0 else nc.vector.tensor_copy)
         flip_hidden(0)
         regroup_wv(0)
         score(0)
-        quantise_wv(0)
         quantise_hidden(0)
+        quantise_wv(0)
         for n in range(2):
             v_rows_of[n] = stream.tile([P, TILES, W], BF16, tag="v_rows", name="v_rows")
 
         for s in range(STEPS):
-            top(s)
+            if s >= PASSES:
+                top_prev(s)
             if s + 1 < STEPS:
                 flip_hidden(s + 1)
+            top_own(s)
             if s >= 1:
                 flip_e(s - 1)
+            if QK_FLIP_STEP <= s < QK_FLIP_STEP + TILES:
+                flipped = psum.tile([P, 2, NH, P], BF16, tag="x_flip", bufs=2)
+                flip_qk(qk_raw, s - QK_FLIP_STEP + TILES, flipped, nc.scalar.copy)
             if s + 1 < PASSES:
                 regroup_wv(s + 1)
-            exponential(s)
             if s >= 1:
                 regroup_e(s - 1)
+            exponential(s)
             if s + 1 < STEPS:
                 quantise_hidden(s + 1)
             if s + 1 < PASSES:
@@ -407,14 +414,16 @@ def tile_localselfattention_pa_k_kernel(tc, q, k_scaled, hidden_states, Wv, out)
                 attend(s // 4 - TILES, 3, True)
             if s + 1 < STEPS:
                 score(s + 1)
-            if s % 2 == 0 and s // 2 + 2 < STEPS // 2:
-                load_hidden(s // 2 + 2)
-                if s + 4 < PASSES:
-                    load_wv(s // 2 + 2)
+            if s % 2 == 0 and s + 4 < PASSES:
+                load_passes(s + 4, 2)
+            if s % 2 == 0 and PASSES <= s + 4 < STEPS:
+                load_half_tile(s + 4)
+            if s == QK_FLIP_STEP - 2:
+                qk_raw = load_qk(1)
 
         flip_e(STEPS - 1)
         regroup_e(STEPS - 1)
         quantise_v(1)
         quantise_e(2 * TILES - 1)
         for j in range(TILES, 2 * TILES):
-            attend(j, j % TILES, j % 2 == 0)
+            attend(j, j % TILES, j % 2 == 1)

@@ -27,7 +27,8 @@ STEPS = 2 * PASSES
 LOAD_COLS = 2 * TILES * K_PASS
 MASKED = -1.0e9
 WV_VECTOR_COLS = 368
-QK_FLIP_STEP = 8
+LEAD = 4
+assert LEAD == TILES
 
 FLOPS = 2 * S * HID * W + 2 * 2 * NH * 3 * CHUNK * CHUNK * DH
 
@@ -72,6 +73,7 @@ def tile_localselfattention_pa_k_kernel(tc, q, k_scaled, hidden_states, Wv, out)
         e_codes = keep.tile([P, 3 * TILES, W], U32, align_bytes=64)
         e_scales = keep.tile([P, 3 * TILES, W], U8, align_bytes=64)
         den = keep.tile([P, 2 * TILES * NH], F32)
+        one_over_den = keep.tile([P, 2 * TILES * NH], F32)
         own_grouped = []
         for i in range(TILES):
             grouped = keep.tile([P, NH, P, PACK], BF16, name="own_grouped%d" % i, align_bytes=64)
@@ -91,6 +93,7 @@ def tile_localselfattention_pa_k_kernel(tc, q, k_scaled, hidden_states, Wv, out)
         e_flip_of = {}
         prev_grouped_of = {}
         v_rows_of = {}
+        v_grouped_of = {}
 
         def load_qk(n):
             raw = stream.tile([P, LOAD_COLS], BF16, tag="x_raw", bufs=4)
@@ -208,16 +211,19 @@ def tile_localselfattention_pa_k_kernel(tc, q, k_scaled, hidden_states, Wv, out)
             n, t = divmod(tile_of_positions, TILES)
             copy(out=v_rows_of[n][:, t, :], in_=accs[tile_of_positions][:])
 
-        def quantise_v(n):
+        def regroup_v(n):
             v_grouped = stream.tile([P, W, PACK], BF16, tag="v_grouped", bufs=1, align_bytes=64)
+            v_grouped_of[n] = v_grouped
             nc.vector.tensor_copy(
                 out=v_grouped[:].rearrange("p (c i) t -> p c t i", i=4),
                 in_=v_rows_of[n][:].rearrange("p t (c i) -> p c t i", i=4),
             )
+
+        def quantise_v(n):
             nc.vector.quantize_mx(
                 out=v_codes[:, n, :].bitcast(FP8X4),
                 scales=v_scales[:, n, :],
-                in_=v_grouped[:].rearrange("p c t -> p (c t)"),
+                in_=v_grouped_of[n][:].rearrange("p c t -> p (c t)"),
             )
 
         def score(s):
@@ -311,6 +317,8 @@ def tile_localselfattention_pa_k_kernel(tc, q, k_scaled, hidden_states, Wv, out)
 
         def quantise_e(j):
             n, i = divmod(j, TILES)
+            heads = slice(j * NH, (j + 1) * NH)
+            nc.vector.reciprocal(out=one_over_den[:, heads], in_=den[:, heads])
             nc.vector.quantize_mx(
                 out=e_codes[:, j, :].bitcast(FP8X4),
                 scales=e_scales[:, j, :],
@@ -347,14 +355,13 @@ def tile_localselfattention_pa_k_kernel(tc, q, k_scaled, hidden_states, Wv, out)
                         start=False,
                         stop=True,
                     )
-            recip = stream.tile([P, NH], F32, tag="recip")
-            nc.vector.reciprocal(out=recip[:], in_=den[:, j * NH : (j + 1) * NH])
-            o_sb = stream.tile([P, NH, DH], F32, tag="o_sb")
+            recip = one_over_den[:, j * NH : (j + 1) * NH]
+            o_sb = stream.tile([P, NH, DH], F32, tag="o_sb", bufs=4)
             if on_vector:
                 nc.vector.tensor_tensor(
                     out=o_sb[:],
                     in0=o[:].rearrange("p (h d) -> p h d", h=NH),
-                    in1=recip[:].unsqueeze(2).to_broadcast([P, NH, DH]),
+                    in1=recip.unsqueeze(2).to_broadcast([P, NH, DH]),
                     op=ALU.mult,
                 )
             else:
@@ -364,6 +371,13 @@ def tile_localselfattention_pa_k_kernel(tc, q, k_scaled, hidden_states, Wv, out)
                     )
             nc.sync.dma_start(out=out_rows[j * P : (j + 1) * P, :], in_=o_sb[:].rearrange("p h d -> p (h d)"))
 
+        def softmax_of(s):
+            if -LEAD <= s < PASSES - LEAD:
+                return s + LEAD
+            if PASSES <= s < STEPS:
+                return s
+            return None
+
         qk_raw = load_qk(0)
         load_passes(0, 1)
         load_passes(1, 1)
@@ -371,58 +385,62 @@ def tile_localselfattention_pa_k_kernel(tc, q, k_scaled, hidden_states, Wv, out)
         for t in range(TILES):
             flipped = psum.tile([P, 2, NH, P], BF16, tag="bank%d" % t)
             flip_qk(qk_raw, t, flipped, nc.scalar.copy if t % 2 == 0 else nc.vector.tensor_copy)
-        flip_hidden(0)
-        regroup_wv(0)
         score(0)
-        quantise_hidden(0)
-        quantise_wv(0)
         for n in range(2):
             v_rows_of[n] = stream.tile([P, TILES, W], BF16, tag="v_rows", name="v_rows")
 
-        for s in range(STEPS):
-            if s >= PASSES:
-                top_prev(s)
-            if s + 1 < STEPS:
+        for s in range(-LEAD, STEPS):
+            before, now, after = softmax_of(s - 1), softmax_of(s), softmax_of(s + 1)
+            if now is not None and now >= PASSES:
+                top_prev(now)
+            if 0 <= s + 1 < STEPS:
                 flip_hidden(s + 1)
-            top_own(s)
-            if s >= 1:
-                flip_e(s - 1)
-            if QK_FLIP_STEP <= s < QK_FLIP_STEP + TILES:
-                flipped = psum.tile([P, 2, NH, P], BF16, tag="x_flip", bufs=2)
-                flip_qk(qk_raw, s - QK_FLIP_STEP + TILES, flipped, nc.scalar.copy)
-            if s + 1 < PASSES:
+            if now is not None:
+                top_own(now)
+            if before is not None:
+                flip_e(before)
+            if PASSES - LEAD <= s < PASSES:
+                flipped = psum.tile([P, 2, NH, P], BF16, tag="s_own")
+                flip_qk(qk_raw, s - PASSES + LEAD + TILES, flipped, nc.scalar.copy)
+            if 0 <= s + 1 < PASSES:
                 regroup_wv(s + 1)
-            if s >= 1:
-                regroup_e(s - 1)
-            exponential(s)
-            if s + 1 < STEPS:
+            if before is not None:
+                regroup_e(before)
+            if now is not None:
+                exponential(now)
+            if 0 <= s + 1 < STEPS:
                 quantise_hidden(s + 1)
-            if s + 1 < PASSES:
+            if 0 <= s + 1 < PASSES:
                 quantise_wv(s + 1)
-            if s >= NH and s % NH == 0:
-                quantise_e(s // NH - 1)
+            if before is not None and before % NH == NH - 1:
+                quantise_e(before // NH)
             if s == PASSES:
+                regroup_v(0)
+            if s == PASSES + 1:
                 quantise_v(0)
-            project(s)
+            if s >= 0:
+                project(s)
             if s == PASSES - 1:
                 round_v(2, nc.scalar.copy)
                 round_v(1, nc.vector.tensor_copy)
                 round_v(0, nc.scalar.copy)
                 round_v(3, nc.vector.tensor_copy)
-            if s >= PASSES and s % 4 == 3:
-                round_v(s // 4, nc.scalar.copy)
+            if s >= PASSES and s % 4 == 2:
                 attend(s // 4 - TILES, 3, True)
-            if s + 1 < STEPS:
-                score(s + 1)
-            if s % 2 == 0 and s + 4 < PASSES:
+            if s >= PASSES and s % 4 == 3:
+                round_v(s // 4, nc.vector.tensor_copy)
+            if after is not None:
+                score(after)
+            if s >= 0 and s % 2 == 0 and s + 4 < PASSES:
                 load_passes(s + 4, 2)
             if s % 2 == 0 and PASSES <= s + 4 < STEPS:
                 load_half_tile(s + 4)
-            if s == QK_FLIP_STEP - 2:
+            if s == PASSES - 2 * LEAD:
                 qk_raw = load_qk(1)
 
         flip_e(STEPS - 1)
         regroup_e(STEPS - 1)
+        regroup_v(1)
         quantise_v(1)
         quantise_e(2 * TILES - 1)
         for j in range(TILES, 2 * TILES):

@@ -22,11 +22,14 @@ W = NH * DH
 CHUNK = 512
 TILES = CHUNK // P
 PASSES = HID // K_PASS
+PAIRS = 4
+STEPS = 2 * TILES * PASSES // PAIRS
 WORDS = K_PASS // 2
-STEPS = 2 * PASSES
-LOAD_COLS = 2 * TILES * K_PASS
+LOAD_COLS = 2 * PAIRS * K_PASS
+RUN = 4
 MASKED = -1.0e9
-WV_VECTOR_COLS = 368
+WV_VECTOR_COLS = 400
+LOAD_AHEAD = 4
 LEAD = 4
 assert LEAD == TILES
 
@@ -104,15 +107,6 @@ def tile_localselfattention_pa_k_kernel(tc, q, k_scaled, hidden_states, Wv, out)
                 )
             return qk_raw
 
-        def flip_qk(qk_raw, tile_of_positions, flipped, copy):
-            t = tile_of_positions % TILES
-            for o in range(2):
-                for h in range(NH):
-                    nc.tensor.transpose(flipped[:, o, h, :], qk_raw[:, o, t, h * DH : (h + 1) * DH], ident_bf[:])
-            positions = slice(tile_of_positions * P, (tile_of_positions + 1) * P)
-            copy(out=q_flipped[:, :, positions], in_=flipped[:, 0, :, :])
-            copy(out=k_flipped[:, :, positions], in_=flipped[:, 1, :, :])
-
         def load_passes(g, count):
             x_raw = stream.tile([P, LOAD_COLS], BF16, tag="x_raw", bufs=4)
             used = x_raw[:, : TILES * count * K_PASS]
@@ -132,23 +126,36 @@ def tile_localselfattention_pa_k_kernel(tc, q, k_scaled, hidden_states, Wv, out)
 
         def load_half_tile(s):
             x_raw = stream.tile([P, LOAD_COLS], BF16, tag="x_raw", bufs=4)
-            j, b = divmod(s // 2, 2)
-            nc.sync.dma_start(out=x_raw[:], in_=x_rows[j * P : (j + 1) * P, b * LOAD_COLS : (b + 1) * LOAD_COLS])
+            tile_of_positions, first_pass = divmod(s * PAIRS, PASSES)
+            first_col = first_pass * K_PASS
+            nc.sync.dma_start(
+                out=x_raw[:],
+                in_=x_rows[tile_of_positions * P : (tile_of_positions + 1) * P, first_col : first_col + LOAD_COLS],
+            )
             words = x_raw[:].bitcast(F32).rearrange("p (g w) -> p g w", w=WORDS)
             for local in range(2):
-                x_blocks[s + local] = [words[:, 4 * local + r, :] for r in range(4)]
+                x_blocks[s + local] = [words[:, PAIRS * local + r, :] for r in range(PAIRS)]
+
+        def flip_qk(qk_raw, tile_of_positions, flipped, copy):
+            t = tile_of_positions % TILES
+            for o in range(2):
+                for h in range(NH):
+                    nc.tensor.transpose(flipped[:, o, h, :], qk_raw[:, o, t, h * DH : (h + 1) * DH], ident_bf[:])
+            positions = slice(tile_of_positions * P, (tile_of_positions + 1) * P)
+            copy(out=q_flipped[:, :, positions], in_=flipped[:, 0, :, :])
+            copy(out=k_flipped[:, :, positions], in_=flipped[:, 1, :, :])
 
         def regroup_wv(g):
             w_grouped = stream.tile([P, W, PACK], BF16, tag="w_grouped", align_bytes=64)
             w_grouped_of[g] = w_grouped
             cut = WV_VECTOR_COLS
             nc.vector.tensor_copy(
-                out=w_grouped[:, :cut, :].rearrange("p (c i) t -> p c t i", i=4),
-                in_=w_passes[g][:, :, :cut].rearrange("p t (c i) -> p c t i", i=4),
+                out=w_grouped[:, :cut, :].rearrange("p (c i) t -> p c t i", i=RUN),
+                in_=w_passes[g][:, :, :cut].rearrange("p t (c i) -> p c t i", i=RUN),
             )
             nc.scalar.copy(
-                out=w_grouped[:, cut:, :].rearrange("p (c i) t -> p c t i", i=4),
-                in_=w_passes[g][:, :, cut:].rearrange("p t (c i) -> p c t i", i=4),
+                out=w_grouped[:, cut:, :].rearrange("p (c i) t -> p c t i", i=RUN),
+                in_=w_passes[g][:, :, cut:].rearrange("p t (c i) -> p c t i", i=RUN),
             )
 
         def quantise_wv(g):
@@ -159,9 +166,9 @@ def tile_localselfattention_pa_k_kernel(tc, q, k_scaled, hidden_states, Wv, out)
             )
 
         def flip_hidden(s):
-            x_grouped = stream.tile([P, 4 * P * PACK], BF16, tag="x_grouped", align_bytes=64)
+            x_grouped = stream.tile([P, PAIRS * P * PACK], BF16, tag="x_grouped", align_bytes=64)
             x_grouped_of[s] = x_grouped
-            grouped_words = x_grouped[:].bitcast(F32).rearrange("p (r q u) -> p r q u", r=4, u=2)
+            grouped_words = x_grouped[:].bitcast(F32).rearrange("p (r q u) -> p r q u", r=PAIRS, u=2)
             for half in range(2):
                 flipped = psum.tile([P, 2, 2, P], F32, tag="x_flip", bufs=2)
                 for r in range(2):
@@ -177,24 +184,22 @@ def tile_localselfattention_pa_k_kernel(tc, q, k_scaled, hidden_states, Wv, out)
                     nc.vector.tensor_copy(out=dst, in_=src)
 
         def quantise_hidden(s):
-            x_codes = stream.tile([P, 4 * P], U32, tag="x_codes", bufs=3, align_bytes=64)
-            x_scales = stream.tile([P, 4 * P], U8, tag="x_scales", bufs=3, align_bytes=64)
+            x_codes = stream.tile([P, PAIRS * P], U32, tag="x_codes", bufs=3, align_bytes=64)
+            x_scales = stream.tile([P, PAIRS * P], U8, tag="x_scales", bufs=3, align_bytes=64)
             nc.vector.quantize_mx(out=x_codes[:].bitcast(FP8X4), scales=x_scales[:], in_=x_grouped_of[s][:])
             x_quantised[s] = (x_codes, x_scales)
 
         def project(s):
             x_codes, x_scales = x_quantised[s]
-            for r in range(4):
+            for r in range(PAIRS):
                 if s < PASSES:
-                    tile_of_positions, g = r, s
+                    tile_of_positions, g, bank = r, s, r
                 else:
-                    tile_of_positions, g = s // 4, 4 * (s % 4) + r
+                    tile_of_positions, g = divmod(s * PAIRS + r, PASSES)
+                    bank = tile_of_positions % 2
                 if g == 0:
                     accs[tile_of_positions] = psum.tile(
-                        [P, W],
-                        F32,
-                        tag="bank%d" % (r if s < PASSES else tile_of_positions % 2),
-                        name="acc%d" % tile_of_positions,
+                        [P, W], F32, tag="bank%d" % bank, name="acc%d" % tile_of_positions
                     )
                 cols = slice(r * P, (r + 1) * P)
                 nc.tensor.matmul_mx(
@@ -214,20 +219,24 @@ def tile_localselfattention_pa_k_kernel(tc, q, k_scaled, hidden_states, Wv, out)
         def regroup_v(n):
             v_grouped = stream.tile([P, W, PACK], BF16, tag="v_grouped", bufs=1, align_bytes=64)
             v_grouped_of[n] = v_grouped
-            nc.vector.tensor_copy(
-                out=v_grouped[:].rearrange("p (c i) t -> p c t i", i=4),
-                in_=v_rows_of[n][:].rearrange("p t (c i) -> p c t i", i=4),
-            )
+            for half in range(2):
+                cols = slice(half * W // 2, (half + 1) * W // 2)
+                nc.vector.tensor_copy(
+                    out=v_grouped[:, cols, :].rearrange("p (c i) t -> p c t i", i=RUN),
+                    in_=v_rows_of[n][:, :, cols].rearrange("p t (c i) -> p c t i", i=RUN),
+                )
 
         def quantise_v(n):
-            nc.vector.quantize_mx(
-                out=v_codes[:, n, :].bitcast(FP8X4),
-                scales=v_scales[:, n, :],
-                in_=v_grouped_of[n][:].rearrange("p c t -> p (c t)"),
-            )
+            for half in range(2):
+                cols = slice(half * W // 2, (half + 1) * W // 2)
+                nc.vector.quantize_mx(
+                    out=v_codes[:, n, cols].bitcast(FP8X4),
+                    scales=v_scales[:, n, cols],
+                    in_=v_grouped_of[n][:, cols, :].rearrange("p c t -> p (c t)"),
+                )
 
-        def score(s):
-            j, h = divmod(s, NH)
+        def score(u):
+            j, h = divmod(u, NH)
             n, i = divmod(j, TILES)
             own = (i + 1) * P
             queries = q_flipped[:, h, j * P : (j + 1) * P]
@@ -243,15 +252,15 @@ def tile_localselfattention_pa_k_kernel(tc, q, k_scaled, hidden_states, Wv, out)
                 nc.tensor.matmul(
                     s_prev[:], lhsT=queries, rhs=k_flipped[:, h, (n - 1) * CHUNK : n * CHUNK], start=True, stop=True
                 )
-            scores_psum[s] = (s_own, s_prev)
+            scores_psum[u] = (s_own, s_prev)
 
-        def top_prev(s):
+        def top_prev(u):
             minus_scores = stream.tile([P, 2 * CHUNK], F32, tag="minus_scores")
             minus_top = stream.tile([P, 2], F32, tag="minus_top")
-            scores_of[s] = (minus_scores, minus_top)
+            scores_of[u] = (minus_scores, minus_top)
             nc.vector.tensor_scalar(
                 out=minus_scores[:, :CHUNK],
-                in0=scores_psum[s][1][:],
+                in0=scores_psum[u][1][:],
                 scalar1=-1.0,
                 scalar2=None,
                 op0=ALU.mult,
@@ -259,17 +268,17 @@ def tile_localselfattention_pa_k_kernel(tc, q, k_scaled, hidden_states, Wv, out)
                 accum_out=minus_top[:, 0:1],
             )
 
-        def top_own(s):
-            n, i = divmod(s // NH, TILES)
+        def top_own(u):
+            n, i = divmod(u // NH, TILES)
             own = (i + 1) * P
             if n == 0:
                 minus_scores = stream.tile([P, 2 * CHUNK], F32, tag="minus_scores")
                 minus_top = stream.tile([P, 2], F32, tag="minus_top")
-                scores_of[s] = (minus_scores, minus_top)
-            minus_scores, minus_top = scores_of[s]
+                scores_of[u] = (minus_scores, minus_top)
+            minus_scores, minus_top = scores_of[u]
             nc.vector.tensor_scalar(
                 out=minus_scores[:, CHUNK : CHUNK + own],
-                in0=scores_psum[s][0][:, :own],
+                in0=scores_psum[u][0][:, :own],
                 scalar1=-1.0,
                 scalar2=(minus_top[:, 0:1] if n > 0 else None),
                 op0=ALU.mult,
@@ -277,11 +286,11 @@ def tile_localselfattention_pa_k_kernel(tc, q, k_scaled, hidden_states, Wv, out)
                 accum_out=minus_top[:, 1:2],
             )
 
-        def exponential(s):
-            n, i = divmod(s // NH, TILES)
+        def exponential(u):
+            n, i = divmod(u // NH, TILES)
             first = CHUNK * (1 - n)
             last = CHUNK + (i + 1) * P
-            minus_scores, minus_top = scores_of[s]
+            minus_scores, minus_top = scores_of[u]
             e = stream.tile([P, 2 * CHUNK], BF16, tag="e")
             nc.scalar.activation(
                 out=e[:, first:last],
@@ -289,21 +298,21 @@ def tile_localselfattention_pa_k_kernel(tc, q, k_scaled, hidden_states, Wv, out)
                 func=ACT.Exp,
                 bias=minus_top[:, 1:2],
                 scale=-1.0,
-                accum_out=den[:, s : s + 1],
+                accum_out=den[:, u : u + 1],
             )
-            e_of[s] = e
+            e_of[u] = e
 
-        def flip_e(s):
-            n, i = divmod(s // NH, TILES)
+        def flip_e(u):
+            n, i = divmod(u // NH, TILES)
             e_flip = psum.tile([P, 2 * TILES, P], BF16, tag="e_flip")
             for b in range(TILES * (1 - n), TILES + i + 1):
-                nc.tensor.transpose(e_flip[:, b, :], e_of[s][:, b * P : (b + 1) * P], ident_bf[:])
-            e_flip_of[s] = e_flip
+                nc.tensor.transpose(e_flip[:, b, :], e_of[u][:, b * P : (b + 1) * P], ident_bf[:])
+            e_flip_of[u] = e_flip
 
-        def regroup_e(s):
-            j, h = divmod(s, NH)
+        def regroup_e(u):
+            j, h = divmod(u, NH)
             n, i = divmod(j, TILES)
-            e_flip = e_flip_of[s]
+            e_flip = e_flip_of[u]
             nc.scalar.copy(
                 out=own_grouped[i][:, h, :, : i + 1],
                 in_=e_flip[:, TILES : TILES + i + 1, :].rearrange("p t q -> p q t"),
@@ -389,8 +398,15 @@ def tile_localselfattention_pa_k_kernel(tc, q, k_scaled, hidden_states, Wv, out)
         for n in range(2):
             v_rows_of[n] = stream.tile([P, TILES, W], BF16, tag="v_rows", name="v_rows")
 
+        steps_of_a_tile = PASSES // PAIRS
         for s in range(-LEAD, STEPS):
             before, now, after = softmax_of(s - 1), softmax_of(s), softmax_of(s + 1)
+            if s >= 0 and s % 2 == 0 and s + LOAD_AHEAD < PASSES:
+                load_passes(s + LOAD_AHEAD, 2)
+            if s % 2 == 0 and PASSES <= s + LOAD_AHEAD < STEPS:
+                load_half_tile(s + LOAD_AHEAD)
+            if s == PASSES - 2 * LEAD:
+                qk_raw = load_qk(1)
             if now is not None and now >= PASSES:
                 top_prev(now)
             if 0 <= s + 1 < STEPS:
@@ -425,18 +441,12 @@ def tile_localselfattention_pa_k_kernel(tc, q, k_scaled, hidden_states, Wv, out)
                 round_v(1, nc.vector.tensor_copy)
                 round_v(0, nc.scalar.copy)
                 round_v(3, nc.vector.tensor_copy)
-            if s >= PASSES and s % 4 == 2:
-                attend(s // 4 - TILES, 3, True)
-            if s >= PASSES and s % 4 == 3:
-                round_v(s // 4, nc.vector.tensor_copy)
+            if s >= PASSES and s % steps_of_a_tile == steps_of_a_tile - 2:
+                attend(s // steps_of_a_tile - TILES, 3, True)
+            if s >= PASSES and s % steps_of_a_tile == steps_of_a_tile - 1:
+                round_v(s // steps_of_a_tile, nc.vector.tensor_copy)
             if after is not None:
                 score(after)
-            if s >= 0 and s % 2 == 0 and s + 4 < PASSES:
-                load_passes(s + 4, 2)
-            if s % 2 == 0 and PASSES <= s + 4 < STEPS:
-                load_half_tile(s + 4)
-            if s == PASSES - 2 * LEAD:
-                qk_raw = load_qk(1)
 
         flip_e(STEPS - 1)
         regroup_e(STEPS - 1)

@@ -235,8 +235,12 @@ def tile_localselfattention_pa_k_kernel(tc, q, k_scaled, hidden_states, Wv, out)
                     in_=v_grouped_of[n][:, cols, :].rearrange("p c t -> p (c t)"),
                 )
 
-        def score(u):
+        def tile_and_head(u):
             j, h = divmod(u, NH)
+            return (j if j < TILES else 3 * TILES - 1 - j), h
+
+        def score(u):
+            j, h = tile_and_head(u)
             n, i = divmod(j, TILES)
             own = (i + 1) * P
             queries = q_flipped[:, h, j * P : (j + 1) * P]
@@ -269,7 +273,7 @@ def tile_localselfattention_pa_k_kernel(tc, q, k_scaled, hidden_states, Wv, out)
             )
 
         def top_own(u):
-            n, i = divmod(u // NH, TILES)
+            n, i = divmod(tile_and_head(u)[0], TILES)
             own = (i + 1) * P
             if n == 0:
                 minus_scores = stream.tile([P, 2 * CHUNK], F32, tag="minus_scores")
@@ -287,30 +291,31 @@ def tile_localselfattention_pa_k_kernel(tc, q, k_scaled, hidden_states, Wv, out)
             )
 
         def exponential(u):
-            n, i = divmod(u // NH, TILES)
+            j, h = tile_and_head(u)
+            n, i = divmod(j, TILES)
             first = CHUNK * (1 - n)
             last = CHUNK + (i + 1) * P
             minus_scores, minus_top = scores_of[u]
-            e = stream.tile([P, 2 * CHUNK], BF16, tag="e")
+            e = stream.tile([P, 2 * CHUNK], BF16, tag="e", bufs=3)
             nc.scalar.activation(
                 out=e[:, first:last],
                 in_=minus_scores[:, first:last],
                 func=ACT.Exp,
                 bias=minus_top[:, 1:2],
                 scale=-1.0,
-                accum_out=den[:, u : u + 1],
+                accum_out=den[:, j * NH + h : j * NH + h + 1],
             )
             e_of[u] = e
 
         def flip_e(u):
-            n, i = divmod(u // NH, TILES)
+            n, i = divmod(tile_and_head(u)[0], TILES)
             e_flip = psum.tile([P, 2 * TILES, P], BF16, tag="e_flip")
             for b in range(TILES * (1 - n), TILES + i + 1):
                 nc.tensor.transpose(e_flip[:, b, :], e_of[u][:, b * P : (b + 1) * P], ident_bf[:])
             e_flip_of[u] = e_flip
 
         def regroup_e(u):
-            j, h = divmod(u, NH)
+            j, h = tile_and_head(u)
             n, i = divmod(j, TILES)
             e_flip = e_flip_of[u]
             nc.scalar.copy(
@@ -400,7 +405,7 @@ def tile_localselfattention_pa_k_kernel(tc, q, k_scaled, hidden_states, Wv, out)
 
         steps_of_a_tile = PASSES // PAIRS
         for s in range(-LEAD, STEPS):
-            before, now, after = softmax_of(s - 1), softmax_of(s), softmax_of(s + 1)
+            before, now, after = softmax_of(s - 2), softmax_of(s), softmax_of(s + 1)
             if s >= 0 and s % 2 == 0 and s + LOAD_AHEAD < PASSES:
                 load_passes(s + LOAD_AHEAD, 2)
             if s % 2 == 0 and PASSES <= s + LOAD_AHEAD < STEPS:
@@ -429,7 +434,7 @@ def tile_localselfattention_pa_k_kernel(tc, q, k_scaled, hidden_states, Wv, out)
             if 0 <= s + 1 < PASSES:
                 quantise_wv(s + 1)
             if before is not None and before % NH == NH - 1:
-                quantise_e(before // NH)
+                quantise_e(tile_and_head(before)[0])
             if s == PASSES:
                 regroup_v(0)
             if s == PASSES + 1:
@@ -448,10 +453,11 @@ def tile_localselfattention_pa_k_kernel(tc, q, k_scaled, hidden_states, Wv, out)
             if after is not None:
                 score(after)
 
-        flip_e(STEPS - 1)
-        regroup_e(STEPS - 1)
+        for u in (STEPS - 2, STEPS - 1):
+            flip_e(u)
+            regroup_e(u)
         regroup_v(1)
         quantise_v(1)
-        quantise_e(2 * TILES - 1)
-        for j in range(TILES, 2 * TILES):
-            attend(j, j % TILES, j % 2 == 1)
+        quantise_e(tile_and_head(STEPS - 1)[0])
+        for j in reversed(range(TILES, 2 * TILES)):
+            attend(j, j % TILES, j % 2 == 0)

@@ -30,8 +30,7 @@ RUN = 4
 MASKED = -1.0e9
 WV_VECTOR_COLS = 400
 LOAD_AHEAD = 4
-LEAD = 4
-assert LEAD == TILES
+
 
 FLOPS = 2 * S * HID * W + 2 * 2 * NH * 3 * CHUNK * CHUNK * DH
 
@@ -81,7 +80,7 @@ def tile_localselfattention_pa_k_kernel(tc, q, k_scaled, hidden_states, Wv, out)
         for i in range(TILES):
             grouped = keep.tile([P, NH, P, PACK], BF16, name="own_grouped%d" % i, align_bytes=64)
             if i < TILES - 1:
-                nc.vector.memset(grouped[:], 0.0)
+                nc.gpsimd.memset(grouped[:].rearrange("p h q t -> p (h q t)").bitcast(mybir.dt.int32), 0)
             own_grouped.append(grouped)
 
         x_blocks = {}
@@ -98,24 +97,24 @@ def tile_localselfattention_pa_k_kernel(tc, q, k_scaled, hidden_states, Wv, out)
         v_rows_of = {}
         v_grouped_of = {}
 
-        def load_qk(n):
-            raw = stream.tile([P, LOAD_COLS], BF16, tag="x_raw", bufs=4)
-            qk_raw = raw[:].rearrange("p (o t w) -> p o t w", o=2, w=W)
+        def new_raw():
+            return stream.tile([P, LOAD_COLS], BF16, tag="x_raw", name="x_raw", bufs=5)
+
+        def load_qk(qk_raw, n, first, last):
             for o, rows in enumerate((q_rows, k_rows)):
                 nc.sync.dma_start(
-                    out=qk_raw[:, o, :, :], in_=rows[n * CHUNK : (n + 1) * CHUNK, :].rearrange("(t p) w -> p t w", p=P)
+                    out=qk_raw[:, o, first:last, :],
+                    in_=rows[n * CHUNK + first * P : n * CHUNK + last * P, :].rearrange("(t p) w -> p t w", p=P),
                 )
-            return qk_raw
 
-        def load_passes(g, count):
-            x_raw = stream.tile([P, LOAD_COLS], BF16, tag="x_raw", bufs=4)
+        def load_passes(x_raw, g, count):
             used = x_raw[:, : TILES * count * K_PASS]
             nc.sync.dma_start(
                 out=used.rearrange("p (t k) -> p t k", t=TILES),
                 in_=x_rows[0:CHUNK, g * K_PASS : (g + count) * K_PASS].rearrange("(t p) k -> p t k", p=P),
             )
             words = used.bitcast(F32).rearrange("p (t g w) -> p t g w", t=TILES, w=WORDS)
-            w_raw = stream.tile([P, 2 * PACK, W], BF16, tag="w_raw", bufs=3)
+            w_raw = stream.tile([P, 2 * PACK, W], BF16, tag="w_raw", bufs=4)
             nc.sync.dma_start(
                 out=w_raw[:, : count * PACK, :].rearrange("p (s e) c -> p s (e c)", e=2),
                 in_=Wv[g * K_PASS : (g + count) * K_PASS, :].rearrange("(s p e) c -> p s (e c)", p=P, e=2),
@@ -125,7 +124,7 @@ def tile_localselfattention_pa_k_kernel(tc, q, k_scaled, hidden_states, Wv, out)
                 w_passes[g + local] = w_raw[:, local * PACK : (local + 1) * PACK, :]
 
         def load_half_tile(s):
-            x_raw = stream.tile([P, LOAD_COLS], BF16, tag="x_raw", bufs=4)
+            x_raw = new_raw()
             tile_of_positions, first_pass = divmod(s * PAIRS, PASSES)
             first_col = first_pass * K_PASS
             nc.sync.dma_start(
@@ -136,14 +135,13 @@ def tile_localselfattention_pa_k_kernel(tc, q, k_scaled, hidden_states, Wv, out)
             for local in range(2):
                 x_blocks[s + local] = [words[:, PAIRS * local + r, :] for r in range(PAIRS)]
 
-        def flip_qk(qk_raw, tile_of_positions, flipped, copy):
-            t = tile_of_positions % TILES
-            for o in range(2):
+        def flip_qk(qk_raw, blocks, flipped, copies):
+            for b, (o, j) in enumerate(blocks):
                 for h in range(NH):
-                    nc.tensor.transpose(flipped[:, o, h, :], qk_raw[:, o, t, h * DH : (h + 1) * DH], ident_bf[:])
-            positions = slice(tile_of_positions * P, (tile_of_positions + 1) * P)
-            copy(out=q_flipped[:, :, positions], in_=flipped[:, 0, :, :])
-            copy(out=k_flipped[:, :, positions], in_=flipped[:, 1, :, :])
+                    nc.tensor.transpose(flipped[:, b * NH + h, :], qk_raw[:, o, j % TILES, h * DH : (h + 1) * DH], ident_bf[:])
+            for b, (o, j) in enumerate(blocks):
+                target = (q_flipped, k_flipped)[o]
+                copies[b](out=target[:, :, j * P : (j + 1) * P], in_=flipped[:, b * NH : (b + 1) * NH, :])
 
         def regroup_wv(g):
             w_grouped = stream.tile([P, W, PACK], BF16, tag="w_grouped", align_bytes=64)
@@ -237,7 +235,7 @@ def tile_localselfattention_pa_k_kernel(tc, q, k_scaled, hidden_states, Wv, out)
 
         def tile_and_head(u):
             j, h = divmod(u, NH)
-            return (j if j < TILES else 3 * TILES - 1 - j), h
+            return (j if j <= TILES else 3 * TILES - j), h
 
         def score(u):
             j, h = tile_and_head(u)
@@ -325,7 +323,7 @@ def tile_localselfattention_pa_k_kernel(tc, q, k_scaled, hidden_states, Wv, out)
             if n > 0:
                 if h == 0:
                     prev_grouped_of[j] = stream.tile(
-                        [P, NH, P, PACK], BF16, tag="prev_grouped", name="prev_grouped", align_bytes=64
+                        [P, NH, P, PACK], BF16, tag="w_grouped", name="prev_grouped", align_bytes=64
                     )
                 nc.scalar.copy(out=prev_grouped_of[j][:, h, :, :], in_=e_flip[:, :TILES, :].rearrange("p t q -> p q t"))
 
@@ -386,32 +384,46 @@ def tile_localselfattention_pa_k_kernel(tc, q, k_scaled, hidden_states, Wv, out)
             nc.sync.dma_start(out=out_rows[j * P : (j + 1) * P, :], in_=o_sb[:].rearrange("p h d -> p (h d)"))
 
         def softmax_of(s):
-            if -LEAD <= s < PASSES - LEAD:
-                return s + LEAD
-            if PASSES <= s < STEPS:
-                return s
-            return None
+            return s if 0 <= s < STEPS else None
 
-        qk_raw = load_qk(0)
-        load_passes(0, 1)
-        load_passes(1, 1)
-        load_passes(2, 2)
-        for t in range(TILES):
-            flipped = psum.tile([P, 2, NH, P], BF16, tag="bank%d" % t)
-            flip_qk(qk_raw, t, flipped, nc.scalar.copy if t % 2 == 0 else nc.vector.tensor_copy)
-        score(0)
+        qk_blocks_of = {
+            -1: ((0, 0), (1, 0)),
+            1: ((0, 1), (1, 1)),
+            2: ((0, 2),),
+            3: ((1, 2),),
+            4: ((0, 3),),
+            5: ((1, 3),),
+            14: ((0, 4),),
+            15: ((1, 4),),
+            16: ((1, 5), (1, 6)),
+            17: ((1, 7), (0, 7)),
+            19: ((0, 6), (0, 5)),
+        }
+        x_raws = [new_raw() for g in range(3)]
+        raw = new_raw()
+        qk_raw = raw[:].rearrange("p (o t w) -> p o t w", o=2, w=W)
+        load_passes(x_raws[0], 0, 1)
+        load_qk(qk_raw, 0, 0, 1)
+        load_passes(x_raws[1], 1, 1)
+        load_passes(x_raws[2], 2, 1)
+        load_qk(qk_raw, 0, 1, TILES)
         for n in range(2):
             v_rows_of[n] = stream.tile([P, TILES, W], BF16, tag="v_rows", name="v_rows")
 
         steps_of_a_tile = PASSES // PAIRS
-        for s in range(-LEAD, STEPS):
+        for s in range(-1, STEPS):
             before, now, after = softmax_of(s - 2), softmax_of(s), softmax_of(s + 1)
+            if s == 0:
+                load_passes(new_raw(), 3, 1)
             if s >= 0 and s % 2 == 0 and s + LOAD_AHEAD < PASSES:
-                load_passes(s + LOAD_AHEAD, 2)
+                load_passes(new_raw(), s + LOAD_AHEAD, 2)
+            if s == PASSES - LOAD_AHEAD:
+                raw = new_raw()
+                qk_raw = raw[:].rearrange("p (o t w) -> p o t w", o=2, w=W)
+                load_qk(qk_raw, 1, 0, 1)
+                load_qk(qk_raw, 1, 1, TILES)
             if s % 2 == 0 and PASSES <= s + LOAD_AHEAD < STEPS:
                 load_half_tile(s + LOAD_AHEAD)
-            if s == PASSES - 2 * LEAD:
-                qk_raw = load_qk(1)
             if now is not None and now >= PASSES:
                 top_prev(now)
             if 0 <= s + 1 < STEPS:
@@ -420,9 +432,15 @@ def tile_localselfattention_pa_k_kernel(tc, q, k_scaled, hidden_states, Wv, out)
                 top_own(now)
             if before is not None:
                 flip_e(before)
-            if PASSES - LEAD <= s < PASSES:
-                flipped = psum.tile([P, 2, NH, P], BF16, tag="s_own")
-                flip_qk(qk_raw, s - PASSES + LEAD + TILES, flipped, nc.scalar.copy)
+            if s in qk_blocks_of:
+                blocks = qk_blocks_of[s]
+                if s >= PASSES:
+                    flipped = psum.tile([P, 2 * NH, P], BF16, tag="bank3", name="qk_flip")
+                elif before is not None:
+                    flipped = e_flip_of[before]
+                else:
+                    flipped = psum.tile([P, 2 * TILES, P], BF16, tag="e_flip", name="qk_flip")
+                flip_qk(qk_raw, blocks, flipped, (nc.scalar.copy, nc.vector.tensor_copy if s < 0 else nc.scalar.copy))
             if 0 <= s + 1 < PASSES:
                 regroup_wv(s + 1)
             if before is not None:
@@ -459,5 +477,5 @@ def tile_localselfattention_pa_k_kernel(tc, q, k_scaled, hidden_states, Wv, out)
         regroup_v(1)
         quantise_v(1)
         quantise_e(tile_and_head(STEPS - 1)[0])
-        for j in reversed(range(TILES, 2 * TILES)):
-            attend(j, j % TILES, j % 2 == 0)
+        for j in (4, 7, 6, 5):
+            attend(j, j % TILES, j % 2 == 1)

@@ -29,7 +29,9 @@ LOAD_COLS = 2 * PAIRS * K_PASS
 RUN = 4
 MASKED = -1.0e9
 WV_VECTOR_COLS = 400
-LOAD_AHEAD = 4
+WV_AHEAD = 5
+HALVES = ((0, 1), (2, 3))
+TILE_ORDER = (0, 1, 2, 3, 4, 5, 7, 6)
 
 
 FLOPS = 2 * S * HID * W + 2 * 2 * NH * 3 * CHUNK * CHUNK * DH
@@ -79,7 +81,7 @@ def tile_localselfattention_pa_k_kernel(tc, q, k_scaled, hidden_states, Wv, out)
         own_grouped = []
         for i in range(TILES):
             grouped = keep.tile([P, NH, P, PACK], BF16, name="own_grouped%d" % i, align_bytes=64)
-            if i < TILES - 1:
+            if i < 2:
                 nc.gpsimd.memset(grouped[:].rearrange("p h q t -> p (h q t)").bitcast(mybir.dt.int32), 0)
             own_grouped.append(grouped)
 
@@ -89,7 +91,8 @@ def tile_localselfattention_pa_k_kernel(tc, q, k_scaled, hidden_states, Wv, out)
         w_grouped_of = {}
         x_quantised = {}
         accs = {}
-        scores_psum = {}
+        s_own_of = {}
+        s_prev_of = {}
         scores_of = {}
         e_of = {}
         e_flip_of = {}
@@ -97,45 +100,54 @@ def tile_localselfattention_pa_k_kernel(tc, q, k_scaled, hidden_states, Wv, out)
         v_rows_of = {}
         v_grouped_of = {}
 
-        def new_raw():
-            return stream.tile([P, LOAD_COLS], BF16, tag="x_raw", name="x_raw", bufs=5)
+        qk_raw = keep.tile([P, 2, TILES, W], BF16)
 
-        def load_qk(qk_raw, n, first, last):
+        def load_qk(first, last):
             for o, rows in enumerate((q_rows, k_rows)):
                 nc.sync.dma_start(
-                    out=qk_raw[:, o, first:last, :],
-                    in_=rows[n * CHUNK + first * P : n * CHUNK + last * P, :].rearrange("(t p) w -> p t w", p=P),
+                    out=qk_raw[:, o, first % TILES : (last - 1) % TILES + 1, :],
+                    in_=rows[first * P : last * P, :].rearrange("(t p) w -> p t w", p=P),
                 )
 
-        def load_passes(x_raw, g, count):
-            used = x_raw[:, : TILES * count * K_PASS]
-            nc.sync.dma_start(
-                out=used.rearrange("p (t k) -> p t k", t=TILES),
-                in_=x_rows[0:CHUNK, g * K_PASS : (g + count) * K_PASS].rearrange("(t p) k -> p t k", p=P),
-            )
-            words = used.bitcast(F32).rearrange("p (t g w) -> p t g w", t=TILES, w=WORDS)
-            w_raw = stream.tile([P, 2 * PACK, W], BF16, tag="w_raw", bufs=4)
-            nc.sync.dma_start(
-                out=w_raw[:, : count * PACK, :].rearrange("p (s e) c -> p s (e c)", e=2),
-                in_=Wv[g * K_PASS : (g + count) * K_PASS, :].rearrange("(s p e) c -> p s (e c)", p=P, e=2),
-            )
+        def load_hidden(g, count):
+            x_raw = stream.tile([P, LOAD_COLS], BF16, tag="x_raw", name="x_raw", bufs=4)
+            used = x_raw[:, : TILES * count * K_PASS].rearrange("p (t k) -> p t k", t=TILES)
+            for u in range(2):
+                nc.sync.dma_start(
+                    out=used[:, 2 * u : 2 * u + 2, :],
+                    in_=x_rows[2 * P * u : 2 * P * (u + 1), g * K_PASS : (g + count) * K_PASS].rearrange("(p e) k -> p e k", e=2),
+                )
             for local in range(count):
-                x_blocks[g + local] = [words[:, t, local, :] for t in range(TILES)]
-                w_passes[g + local] = w_raw[:, local * PACK : (local + 1) * PACK, :]
+                x_blocks[g + local] = [
+                    used[:, t, local * K_PASS : (local + 1) * K_PASS].bitcast(F32) for t in range(TILES)
+                ]
+
+        def load_wv(g):
+            w_raw = stream.tile([P, PACK, W], BF16, tag="w_raw", name="w_raw", bufs=WV_AHEAD)
+            nc.sync.dma_start(
+                out=w_raw[:].rearrange("p (s e) c -> p s (e c)", e=2),
+                in_=Wv[g * K_PASS : (g + 1) * K_PASS, :].rearrange("(s p e) c -> p s (e c)", p=P, e=2),
+            )
+            w_passes[g] = w_raw
 
         def load_half_tile(s):
-            x_raw = new_raw()
+            x_raw = stream.tile([P, LOAD_COLS], BF16, tag="x_raw", name="x_raw", bufs=4)
             tile_of_positions, first_pass = divmod(s * PAIRS, PASSES)
+            first_row = tile_of_positions // 2 * 2 * P
             first_col = first_pass * K_PASS
             nc.sync.dma_start(
                 out=x_raw[:],
-                in_=x_rows[tile_of_positions * P : (tile_of_positions + 1) * P, first_col : first_col + LOAD_COLS],
+                in_=x_rows[first_row : first_row + 2 * P, first_col : first_col + LOAD_COLS].rearrange("(p e) k -> p e k", e=2)[
+                    :, tile_of_positions % 2, :
+                ],
             )
-            words = x_raw[:].bitcast(F32).rearrange("p (g w) -> p g w", w=WORDS)
             for local in range(2):
-                x_blocks[s + local] = [words[:, PAIRS * local + r, :] for r in range(PAIRS)]
+                first = local * PAIRS * K_PASS
+                x_blocks[s + local] = [
+                    x_raw[:, first + r * K_PASS : first + (r + 1) * K_PASS].bitcast(F32) for r in range(PAIRS)
+                ]
 
-        def flip_qk(qk_raw, blocks, flipped, copies):
+        def flip_qk(blocks, flipped, copies):
             for b, (o, j) in enumerate(blocks):
                 for h in range(NH):
                     nc.tensor.transpose(flipped[:, b * NH + h, :], qk_raw[:, o, j % TILES, h * DH : (h + 1) * DH], ident_bf[:])
@@ -182,13 +194,12 @@ def tile_localselfattention_pa_k_kernel(tc, q, k_scaled, hidden_states, Wv, out)
                     nc.vector.tensor_copy(out=dst, in_=src)
 
         def quantise_hidden(s):
-            x_codes = stream.tile([P, PAIRS * P], U32, tag="x_codes", bufs=3, align_bytes=64)
-            x_scales = stream.tile([P, PAIRS * P], U8, tag="x_scales", bufs=3, align_bytes=64)
+            x_codes = stream.tile([P, PAIRS * P], U32, tag="x_codes", bufs=5, align_bytes=64)
+            x_scales = stream.tile([P, PAIRS * P], U8, tag="x_scales", bufs=5, align_bytes=64)
             nc.vector.quantize_mx(out=x_codes[:].bitcast(FP8X4), scales=x_scales[:], in_=x_grouped_of[s][:])
             x_quantised[s] = (x_codes, x_scales)
 
         def project(s):
-            x_codes, x_scales = x_quantised[s]
             for r in range(PAIRS):
                 if s < PASSES:
                     tile_of_positions, g, bank = r, s, r
@@ -199,70 +210,108 @@ def tile_localselfattention_pa_k_kernel(tc, q, k_scaled, hidden_states, Wv, out)
                     accs[tile_of_positions] = psum.tile(
                         [P, W], F32, tag="bank%d" % bank, name="acc%d" % tile_of_positions
                     )
-                cols = slice(r * P, (r + 1) * P)
-                nc.tensor.matmul_mx(
-                    out=accs[tile_of_positions][:],
-                    lhsT=x_codes[:, cols].bitcast(FP8X4),
-                    lhsT_scale=x_scales[:, cols],
-                    rhs=wv_codes[:, g, :].bitcast(FP8X4),
-                    rhs_scale=wv_scales[:, g, :],
-                    start=(g == 0),
-                    stop=(g == PASSES - 1),
-                )
+                last = tile_of_positions == 2 * TILES - 1
+                multiply(accs[tile_of_positions], s, r, g, slice(0, W // 2 if last else W))
+
+        def multiply(acc, s, r, g, out_cols):
+            x_codes, x_scales = x_quantised[s]
+            cols = slice(r * P, (r + 1) * P)
+            nc.tensor.matmul_mx(
+                out=acc[:, out_cols],
+                lhsT=x_codes[:, cols].bitcast(FP8X4),
+                lhsT_scale=x_scales[:, cols],
+                rhs=wv_codes[:, g, out_cols].bitcast(FP8X4),
+                rhs_scale=wv_scales[:, g, out_cols],
+                start=(g == 0),
+                stop=(g == PASSES - 1),
+            )
 
         def round_v(tile_of_positions, copy):
             n, t = divmod(tile_of_positions, TILES)
             copy(out=v_rows_of[n][:, t, :], in_=accs[tile_of_positions][:])
 
-        def regroup_v(n):
-            v_grouped = stream.tile([P, W, PACK], BF16, tag="v_grouped", bufs=1, align_bytes=64)
-            v_grouped_of[n] = v_grouped
-            for half in range(2):
-                cols = slice(half * W // 2, (half + 1) * W // 2)
-                nc.vector.tensor_copy(
-                    out=v_grouped[:, cols, :].rearrange("p (c i) t -> p c t i", i=RUN),
-                    in_=v_rows_of[n][:, :, cols].rearrange("p t (c i) -> p c t i", i=RUN),
-                )
+        def regroup_v(n, half):
+            if half == 0:
+                v_grouped_of[n] = stream.tile([P, W, PACK], BF16, tag="v_grouped", name="v_grouped", bufs=1, align_bytes=64)
+            cols = slice(half * W // 2, (half + 1) * W // 2)
+            nc.vector.tensor_copy(
+                out=v_grouped_of[n][:, cols, :].rearrange("p (c i) t -> p c t i", i=RUN),
+                in_=v_rows_of[n][:, :, cols].rearrange("p t (c i) -> p c t i", i=RUN),
+            )
 
-        def quantise_v(n):
-            for half in range(2):
-                cols = slice(half * W // 2, (half + 1) * W // 2)
-                nc.vector.quantize_mx(
-                    out=v_codes[:, n, cols].bitcast(FP8X4),
-                    scales=v_scales[:, n, cols],
-                    in_=v_grouped_of[n][:, cols, :].rearrange("p c t -> p (c t)"),
-                )
+        def quantise_v(n, half):
+            cols = slice(half * W // 2, (half + 1) * W // 2)
+            nc.vector.quantize_mx(
+                out=v_codes[:, n, cols].bitcast(FP8X4),
+                scales=v_scales[:, n, cols],
+                in_=v_grouped_of[n][:, cols, :].rearrange("p c t -> p (c t)"),
+            )
 
         def tile_and_head(u):
-            j, h = divmod(u, NH)
-            return (j if j <= TILES else 3 * TILES - j), h
+            order, h = divmod(u, NH)
+            return TILE_ORDER[order], h
 
-        def score(u):
+        def place(u):
+            j, h = tile_and_head(u)
+            if j == 0:
+                return 2 * P * h
+            if j == 1:
+                return CHUNK + 2 * P * (h % 2)
+            if j == 2:
+                return CHUNK * (h % 2)
+            return CHUNK
+
+        def first_of_step(u):
+            j, h = tile_and_head(u)
+            return (h if j == 0 else h % 2 if j < 3 else 0) == 0
+
+        def score_own(u):
             j, h = tile_and_head(u)
             n, i = divmod(j, TILES)
             own = (i + 1) * P
             queries = q_flipped[:, h, j * P : (j + 1) * P]
             keys = k_flipped[:, h, n * CHUNK : n * CHUNK + own]
-            s_own = psum.tile([P, CHUNK], F32, tag="s_own")
+            share = (h, h % 2, 0, 0)[i] if n == 0 else 0
+            if share > 0:
+                s_own = s_own_of[u - 1][0]
+            else:
+                s_own = psum.tile([P, CHUNK], F32, tag="s_own", name="s_own")
+            first = share * own
+            s_own_of[u] = (s_own, first)
             if i > 0:
-                nc.tensor.matmul(s_own[:, : i * P], lhsT=queries, rhs=keys[:, : i * P], start=True, stop=True)
-            nc.tensor.matmul(s_own[:, i * P : own], lhsT=ident_bf[:], rhs=later[:], start=True, stop=False)
-            nc.tensor.matmul(s_own[:, i * P : own], lhsT=queries, rhs=keys[:, i * P : own], start=False, stop=True)
-            s_prev = None
-            if n > 0:
-                s_prev = psum.tile([P, CHUNK], F32, tag="bank2")
-                nc.tensor.matmul(
-                    s_prev[:], lhsT=queries, rhs=k_flipped[:, h, (n - 1) * CHUNK : n * CHUNK], start=True, stop=True
-                )
-            scores_psum[u] = (s_own, s_prev)
+                nc.tensor.matmul(s_own[:, first : first + i * P], lhsT=queries, rhs=keys[:, : i * P], start=True, stop=True)
+            diagonal = s_own[:, first + i * P : first + own]
+            nc.tensor.matmul(diagonal, lhsT=ident_bf[:], rhs=later[:], start=True, stop=False)
+            nc.tensor.matmul(diagonal, lhsT=queries, rhs=keys[:, i * P : own], start=False, stop=True)
+
+        def score_prev(u, tag):
+            j, h = tile_and_head(u)
+            n = j // TILES
+            s_prev = psum.tile([P, CHUNK], F32, tag=tag, name="s_prev")
+            nc.tensor.matmul(
+                s_prev[:],
+                lhsT=q_flipped[:, h, j * P : (j + 1) * P],
+                rhs=k_flipped[:, h, (n - 1) * CHUNK : n * CHUNK],
+                start=True,
+                stop=True,
+            )
+            s_prev_of[u] = s_prev
+
+        def scores_tile(u):
+            if u not in scores_of:
+                if first_of_step(u):
+                    minus_scores = stream.tile([P, 2 * CHUNK], F32, tag="minus_scores", name="minus_scores")
+                else:
+                    minus_scores = scores_of[u - 1][0]
+                minus_top = stream.tile([P, 2], F32, tag="minus_top", name="minus_top", bufs=8)
+                scores_of[u] = (minus_scores, minus_top)
+            return scores_of[u]
 
         def top_prev(u):
-            minus_scores = stream.tile([P, 2 * CHUNK], F32, tag="minus_scores")
-            minus_top = stream.tile([P, 2], F32, tag="minus_top")
-            scores_of[u] = (minus_scores, minus_top)
+            minus_scores, minus_top = scores_tile(u)
             nc.vector.tensor_scalar(
                 out=minus_scores[:, :CHUNK],
-                in0=scores_psum[u][1][:],
+                in0=s_prev_of[u][:],
                 scalar1=-1.0,
                 scalar2=None,
                 op0=ALU.mult,
@@ -273,14 +322,11 @@ def tile_localselfattention_pa_k_kernel(tc, q, k_scaled, hidden_states, Wv, out)
         def top_own(u):
             n, i = divmod(tile_and_head(u)[0], TILES)
             own = (i + 1) * P
-            if n == 0:
-                minus_scores = stream.tile([P, 2 * CHUNK], F32, tag="minus_scores")
-                minus_top = stream.tile([P, 2], F32, tag="minus_top")
-                scores_of[u] = (minus_scores, minus_top)
-            minus_scores, minus_top = scores_of[u]
+            minus_scores, minus_top = scores_tile(u)
+            s_own, first = s_own_of[u]
             nc.vector.tensor_scalar(
-                out=minus_scores[:, CHUNK : CHUNK + own],
-                in0=scores_psum[u][0][:, :own],
+                out=minus_scores[:, place(u) : place(u) + own],
+                in0=s_own[:, first : first + own],
                 scalar1=-1.0,
                 scalar2=(minus_top[:, 0:1] if n > 0 else None),
                 op0=ALU.mult,
@@ -291,10 +337,15 @@ def tile_localselfattention_pa_k_kernel(tc, q, k_scaled, hidden_states, Wv, out)
         def exponential(u):
             j, h = tile_and_head(u)
             n, i = divmod(j, TILES)
-            first = CHUNK * (1 - n)
-            last = CHUNK + (i + 1) * P
+            first = 0 if n > 0 else place(u)
+            last = place(u) + (i + 1) * P
             minus_scores, minus_top = scores_of[u]
-            e = stream.tile([P, 2 * CHUNK], BF16, tag="e", bufs=3)
+            if first_of_step(u):
+                e = stream.tile([P, 2 * CHUNK], BF16, tag="e", name="e", bufs=3)
+            else:
+                e = e_of[u - 1]
+            if i % 2 == 0:
+                nc.gpsimd.memset(e[:, last : last + P].bitcast(mybir.dt.int32), 0)
             nc.scalar.activation(
                 out=e[:, first:last],
                 in_=minus_scores[:, first:last],
@@ -307,25 +358,35 @@ def tile_localselfattention_pa_k_kernel(tc, q, k_scaled, hidden_states, Wv, out)
 
         def flip_e(u):
             n, i = divmod(tile_and_head(u)[0], TILES)
-            e_flip = psum.tile([P, 2 * TILES, P], BF16, tag="e_flip")
-            for b in range(TILES * (1 - n), TILES + i + 1):
-                nc.tensor.transpose(e_flip[:, b, :], e_of[u][:, b * P : (b + 1) * P], ident_bf[:])
+            if first_of_step(u):
+                e_flip = psum.tile([P, TILES, P], F32, tag="e_flip", name="e_flip")
+            else:
+                e_flip = e_flip_of[u - 1]
+            words = e_of[u][:].bitcast(F32)
+            own = place(u) // (2 * P)
+            for b in list(range(2 * n)) + list(range(own, own + i // 2 + 1)):
+                nc.tensor.transpose(e_flip[:, b, :], words[:, b * P : (b + 1) * P], ident_f32[:])
             e_flip_of[u] = e_flip
 
         def regroup_e(u):
             j, h = tile_and_head(u)
             n, i = divmod(j, TILES)
             e_flip = e_flip_of[u]
+            own = place(u) // (2 * P)
+            blocks = i // 2 + 1
             nc.scalar.copy(
-                out=own_grouped[i][:, h, :, : i + 1],
-                in_=e_flip[:, TILES : TILES + i + 1, :].rearrange("p t q -> p q t"),
+                out=as_words(own_grouped[i])[:, h, :, :blocks],
+                in_=e_flip[:, own : own + blocks, :].rearrange("p u q -> p q u"),
             )
             if n > 0:
                 if h == 0:
                     prev_grouped_of[j] = stream.tile(
-                        [P, NH, P, PACK], BF16, tag="w_grouped", name="prev_grouped", align_bytes=64
+                        [P, NH, P, PACK], BF16, tag="prev_grouped", name="prev_grouped", align_bytes=64
                     )
-                nc.scalar.copy(out=prev_grouped_of[j][:, h, :, :], in_=e_flip[:, :TILES, :].rearrange("p t q -> p q t"))
+                nc.scalar.copy(out=as_words(prev_grouped_of[j])[:, h, :, :], in_=e_flip[:, :2, :].rearrange("p u q -> p q u"))
+
+        def as_words(grouped):
+            return grouped[:].rearrange("p h q t -> p (h q t)").bitcast(F32).rearrange("p (h q u) -> p h q u", h=NH, u=2)
 
         def quantise_e(j):
             n, i = divmod(j, TILES)
@@ -343,10 +404,9 @@ def tile_localselfattention_pa_k_kernel(tc, q, k_scaled, hidden_states, Wv, out)
                     in_=prev_grouped_of[j][:].rearrange("p h q t -> p (h q t)"),
                 )
 
-        def attend(j, bank, on_vector):
+        def attend(j, heads, o):
             n, i = divmod(j, TILES)
-            o = psum.tile([P, W], F32, tag="bank%d" % bank)
-            for h in range(NH):
+            for h in heads:
                 cols = slice(h * DH, (h + 1) * DH)
                 nc.tensor.matmul_mx(
                     out=o[:, cols],
@@ -367,96 +427,143 @@ def tile_localselfattention_pa_k_kernel(tc, q, k_scaled, hidden_states, Wv, out)
                         start=False,
                         stop=True,
                     )
-            recip = one_over_den[:, j * NH : (j + 1) * NH]
-            o_sb = stream.tile([P, NH, DH], F32, tag="o_sb", bufs=4)
+
+        def divide(j, heads, o, on_vector):
+            cols = slice(heads[0] * DH, (heads[-1] + 1) * DH)
+            recip = one_over_den[:, j * NH + heads[0] : j * NH + heads[-1] + 1]
+            o_sb = stream.tile([P, 2, DH], F32, tag="o_sb", bufs=6)
             if on_vector:
                 nc.vector.tensor_tensor(
                     out=o_sb[:],
-                    in0=o[:].rearrange("p (h d) -> p h d", h=NH),
-                    in1=recip.unsqueeze(2).to_broadcast([P, NH, DH]),
+                    in0=o[:, cols].rearrange("p (h d) -> p h d", d=DH),
+                    in1=recip.unsqueeze(2).to_broadcast([P, len(heads), DH]),
                     op=ALU.mult,
                 )
             else:
-                for h in range(NH):
+                for b, h in enumerate(heads):
                     nc.scalar.activation(
-                        out=o_sb[:, h, :], in_=o[:, h * DH : (h + 1) * DH], func=ACT.Copy, scale=recip[:, h : h + 1]
+                        out=o_sb[:, b, :], in_=o[:, h * DH : (h + 1) * DH], func=ACT.Copy, scale=recip[:, b : b + 1]
                     )
-            nc.sync.dma_start(out=out_rows[j * P : (j + 1) * P, :], in_=o_sb[:].rearrange("p h d -> p (h d)"))
+            nc.sync.dma_start(out=out_rows[j * P : (j + 1) * P, cols], in_=o_sb[:].rearrange("p h d -> p (h d)"))
 
-        def softmax_of(s):
-            return s if 0 <= s < STEPS else None
+        def softmaxes_of(s):
+            if s == -1:
+                return (0, 1, 2, 3)
+            if 0 <= s <= 3:
+                return (2 * s + 4, 2 * s + 5)
+            if 4 <= s <= 11:
+                return (s + 8,)
+            if PASSES <= s < PASSES + 12:
+                return (s + 4,)
+            return ()
+
+        def second(u):
+            j, h = tile_and_head(u)
+            return j == 2 and h % 2 == 1 or j == TILES
 
         qk_blocks_of = {
-            -1: ((0, 0), (1, 0)),
-            1: ((0, 1), (1, 1)),
-            2: ((0, 2),),
-            3: ((1, 2),),
-            4: ((0, 3),),
-            5: ((1, 3),),
-            14: ((0, 4),),
-            15: ((1, 4),),
-            16: ((1, 5), (1, 6)),
-            17: ((1, 7), (0, 7)),
-            19: ((0, 6), (0, 5)),
+            -1: ((0, 2), (1, 2)),
+            0: ((0, 3), (1, 3)),
+            6: ((0, 4),),
+            7: ((1, 4),),
+            8: ((0, 5),),
+            9: ((1, 5),),
+            14: ((1, 6), (1, 7)),
+            15: ((0, 7), (0, 6)),
         }
-        x_raws = [new_raw() for g in range(3)]
-        raw = new_raw()
-        qk_raw = raw[:].rearrange("p (o t w) -> p o t w", o=2, w=W)
-        load_passes(x_raws[0], 0, 1)
-        load_qk(qk_raw, 0, 0, 1)
-        load_passes(x_raws[1], 1, 1)
-        load_passes(x_raws[2], 2, 1)
-        load_qk(qk_raw, 0, 1, TILES)
+
+        load_qk(0, 2)
+        load_hidden(0, 1)
+        load_wv(0)
+        load_qk(2, 4)
+        for g in range(1, 4):
+            load_hidden(g, 1)
+            load_wv(g)
+        load_wv(4)
         for n in range(2):
             v_rows_of[n] = stream.tile([P, TILES, W], BF16, tag="v_rows", name="v_rows")
 
+        loads_of = {
+            0: [lambda: load_hidden(4, 2)],
+            1: [lambda: load_hidden(6, 2), lambda: load_qk(4, 6)],
+            3: [lambda: load_hidden(8, 2)],
+            5: [lambda: load_hidden(10, 2)],
+            7: [lambda: load_hidden(12, 2)],
+            9: [lambda: load_hidden(14, 2)],
+            10: [lambda: load_half_tile(16), lambda: load_qk(6, 8)],
+            11: [lambda: load_half_tile(18)],
+            13: [lambda: load_half_tile(20)],
+            15: [lambda: load_half_tile(22)],
+            17: [lambda: load_half_tile(24)],
+            19: [lambda: load_half_tile(26)],
+            21: [lambda: load_half_tile(28)],
+            23: [lambda: load_half_tile(30)],
+        }
+
+        for j in range(2):
+            room = psum.tile([P, 2 * NH, P], BF16, tag="bank%d" % j, name="qk_flip")
+            flip_qk(((0, j), (1, j)), room, (nc.scalar.copy, nc.vector.tensor_copy))
+        for u in range(NH):
+            score_own(u)
+
         steps_of_a_tile = PASSES // PAIRS
         for s in range(-1, STEPS):
-            before, now, after = softmax_of(s - 2), softmax_of(s), softmax_of(s + 1)
-            if s == 0:
-                load_passes(new_raw(), 3, 1)
-            if s >= 0 and s % 2 == 0 and s + LOAD_AHEAD < PASSES:
-                load_passes(new_raw(), s + LOAD_AHEAD, 2)
-            if s == PASSES - LOAD_AHEAD:
-                raw = new_raw()
-                qk_raw = raw[:].rearrange("p (o t w) -> p o t w", o=2, w=W)
-                load_qk(qk_raw, 1, 0, 1)
-                load_qk(qk_raw, 1, 1, TILES)
-            if s % 2 == 0 and PASSES <= s + LOAD_AHEAD < STEPS:
-                load_half_tile(s + LOAD_AHEAD)
-            if now is not None and now >= PASSES:
-                top_prev(now)
+            before, now, after = softmaxes_of(s - 2), softmaxes_of(s), softmaxes_of(s + 1)
+            for load in loads_of.get(s, []):
+                load()
+            if 0 <= s < PASSES - WV_AHEAD:
+                load_wv(s + WV_AHEAD)
+            for u in now:
+                if tile_and_head(u)[0] >= TILES:
+                    top_prev(u)
+                elif not second(u):
+                    top_own(u)
             if 0 <= s + 1 < STEPS:
                 flip_hidden(s + 1)
-            if now is not None:
-                top_own(now)
-            if before is not None:
-                flip_e(before)
+            for u in now:
+                if tile_and_head(u)[0] >= TILES and not second(u):
+                    top_own(u)
+            for u in before:
+                flip_e(u)
             if s in qk_blocks_of:
-                blocks = qk_blocks_of[s]
-                if s >= PASSES:
-                    flipped = psum.tile([P, 2 * NH, P], BF16, tag="bank3", name="qk_flip")
-                elif before is not None:
-                    flipped = e_flip_of[before]
+                if s == -1:
+                    room = psum.tile([P, 2 * NH, P], BF16, tag="bank2", name="qk_flip")
+                elif s == 0:
+                    room = psum.tile([P, 2 * NH, P], BF16, tag="e_flip", name="qk_flip")
+                elif s >= PASSES:
+                    room = psum.tile([P, 2 * NH, P], BF16, tag=("bank3", "bank1")[s - PASSES], name="qk_flip")
+                elif len(before) > 0:
+                    room = e_flip_of[before[0]][:].rearrange("p b q -> p (b q)").bitcast(BF16).rearrange("p (b q) -> p b q", q=P)
                 else:
-                    flipped = psum.tile([P, 2 * TILES, P], BF16, tag="e_flip", name="qk_flip")
-                flip_qk(qk_raw, blocks, flipped, (nc.scalar.copy, nc.vector.tensor_copy if s < 0 else nc.scalar.copy))
+                    room = psum.tile([P, 2 * NH, P], BF16, tag="e_flip", name="qk_flip")
+                flip_qk(qk_blocks_of[s], room, (nc.scalar.copy, nc.vector.tensor_copy if s < 0 else nc.scalar.copy))
+            for u in now:
+                if second(u):
+                    score_own(u)
             if 0 <= s + 1 < PASSES:
                 regroup_wv(s + 1)
-            if before is not None:
-                regroup_e(before)
-            if now is not None:
-                exponential(now)
+            for u in before:
+                regroup_e(u)
+            for u in now:
+                if not second(u):
+                    exponential(u)
             if 0 <= s + 1 < STEPS:
                 quantise_hidden(s + 1)
+            for u in now:
+                if second(u):
+                    top_own(u)
+                    exponential(u)
             if 0 <= s + 1 < PASSES:
                 quantise_wv(s + 1)
-            if before is not None and before % NH == NH - 1:
-                quantise_e(tile_and_head(before)[0])
+            for u in before:
+                if u % NH == NH - 1:
+                    quantise_e(tile_and_head(u)[0])
             if s == PASSES:
-                regroup_v(0)
+                regroup_v(0, 0)
+                regroup_v(0, 1)
             if s == PASSES + 1:
-                quantise_v(0)
+                quantise_v(0, 0)
+                quantise_v(0, 1)
             if s >= 0:
                 project(s)
             if s == PASSES - 1:
@@ -465,17 +572,32 @@ def tile_localselfattention_pa_k_kernel(tc, q, k_scaled, hidden_states, Wv, out)
                 round_v(0, nc.scalar.copy)
                 round_v(3, nc.vector.tensor_copy)
             if s >= PASSES and s % steps_of_a_tile == steps_of_a_tile - 2:
-                attend(s // steps_of_a_tile - TILES, 3, True)
-            if s >= PASSES and s % steps_of_a_tile == steps_of_a_tile - 1:
-                round_v(s // steps_of_a_tile, nc.vector.tensor_copy)
-            if after is not None:
-                score(after)
+                j = s // steps_of_a_tile - TILES
+                o = psum.tile([P, W], F32, tag="bank3", name="o")
+                attend(j, range(NH), o)
+                for half in HALVES:
+                    divide(j, half, o, False)
+            if PASSES <= s < STEPS - 1 and s % steps_of_a_tile == steps_of_a_tile - 1:
+                round_v(s // steps_of_a_tile, nc.scalar.copy)
+            for u in after:
+                if tile_and_head(u)[0] >= TILES:
+                    score_prev(u, "s_own" if second(u) else "bank2")
+                if not second(u):
+                    score_own(u)
 
-        for u in (STEPS - 2, STEPS - 1):
-            flip_e(u)
-            regroup_e(u)
-        regroup_v(1)
-        quantise_v(1)
-        quantise_e(tile_and_head(STEPS - 1)[0])
-        for j in (4, 7, 6, 5):
-            attend(j, j % TILES, j % 2 == 1)
+        last = 2 * TILES - 1
+        half_cols = [slice(half * W // 2, (half + 1) * W // 2) for half in range(2)]
+        nc.vector.tensor_copy(out=v_rows_of[1][:, TILES - 1, half_cols[0]], in_=accs[last][:, half_cols[0]])
+        regroup_v(1, 0)
+        quantise_v(1, 0)
+        acc = psum.tile([P, W], F32, tag="bank0", name="acc_last")
+        for g in range(PASSES):
+            multiply(acc, STEPS - PASSES // PAIRS + g // PAIRS, g % PAIRS, g, half_cols[1])
+        nc.vector.tensor_copy(out=v_rows_of[1][:, TILES - 1, half_cols[1]], in_=acc[:, half_cols[1]])
+        regroup_v(1, 1)
+        quantise_v(1, 1)
+        for half, tags in enumerate((("bank2", "bank3", "s_own", "e_flip"), ("bank1", "x_flip", "x_flip", "bank0"))):
+            for j, tag in zip(TILE_ORDER[TILES:], tags):
+                o = psum.tile([P, W], F32, tag=tag, name="o", bufs=(2 if tag == "x_flip" else 1))
+                attend(j, HALVES[half], o)
+                divide(j, HALVES[half], o, half == 1 and j % 2 == 0)

@@ -28,7 +28,6 @@ WORDS = K_PASS // 2
 LOAD_COLS = 2 * PAIRS * K_PASS
 RUN = 4
 MASKED = -1.0e9
-WV_VECTOR_COLS = 400
 WV_AHEAD = 5
 HALVES = ((0, 1), (2, 3))
 TILE_ORDER = (0, 1, 2, 3, 4, 5, 7, 6)
@@ -68,8 +67,7 @@ def tile_localselfattention_pa_k_kernel(tc, q, k_scaled, hidden_states, Wv, out)
         later = keep.tile([P, P], BF16)
         nc.vector.tensor_copy(out=later[:], in_=later_f32[:])
 
-        q_flipped = keep.tile([P, NH, S], BF16)
-        k_flipped = keep.tile([P, NH, S], BF16)
+        qk_flipped = keep.tile([P, 2, NH, S], BF16)
         wv_codes = keep.tile([P, PASSES, W], U32, align_bytes=64)
         wv_scales = keep.tile([P, PASSES, W], U8, align_bytes=64)
         v_codes = keep.tile([P, 2, W], U32, align_bytes=64)
@@ -78,12 +76,8 @@ def tile_localselfattention_pa_k_kernel(tc, q, k_scaled, hidden_states, Wv, out)
         e_scales = keep.tile([P, 3 * TILES, W], U8, align_bytes=64)
         den = keep.tile([P, 2 * TILES * NH], F32)
         one_over_den = keep.tile([P, 2 * TILES * NH], F32)
-        own_grouped = []
-        for i in range(TILES):
-            grouped = keep.tile([P, NH, P, PACK], BF16, name="own_grouped%d" % i, align_bytes=64)
-            if i < 2:
-                nc.gpsimd.memset(grouped[:].rearrange("p h q t -> p (h q t)").bitcast(mybir.dt.int32), 0)
-            own_grouped.append(grouped)
+        e_grouped = [keep.tile([P, 2, NH, P, PACK], BF16, name="e_grouped%d" % b, align_bytes=64) for b in range(3)]
+        nc.gpsimd.memset(e_grouped[0][:, 1, :, :, :].rearrange("p h q t -> p (h q t)").bitcast(mybir.dt.int32), 0)
 
         x_blocks = {}
         w_passes = {}
@@ -96,7 +90,6 @@ def tile_localselfattention_pa_k_kernel(tc, q, k_scaled, hidden_states, Wv, out)
         scores_of = {}
         e_of = {}
         e_flip_of = {}
-        prev_grouped_of = {}
         v_rows_of = {}
         v_grouped_of = {}
 
@@ -147,25 +140,21 @@ def tile_localselfattention_pa_k_kernel(tc, q, k_scaled, hidden_states, Wv, out)
                     x_raw[:, first + r * K_PASS : first + (r + 1) * K_PASS].bitcast(F32) for r in range(PAIRS)
                 ]
 
-        def flip_qk(blocks, flipped, copies):
-            for b, (o, j) in enumerate(blocks):
+        def flip_qk(j, which, flipped, copy):
+            for b, o in enumerate(which):
                 for h in range(NH):
                     nc.tensor.transpose(flipped[:, b * NH + h, :], qk_raw[:, o, j % TILES, h * DH : (h + 1) * DH], ident_bf[:])
-            for b, (o, j) in enumerate(blocks):
-                target = (q_flipped, k_flipped)[o]
-                copies[b](out=target[:, :, j * P : (j + 1) * P], in_=flipped[:, b * NH : (b + 1) * NH, :])
+            copy(
+                out=qk_flipped[:, which[0] : which[-1] + 1, :, j * P : (j + 1) * P],
+                in_=flipped[:, : len(which) * NH, :].rearrange("p (o h) q -> p o h q", h=NH),
+            )
 
         def regroup_wv(g):
             w_grouped = stream.tile([P, W, PACK], BF16, tag="w_grouped", align_bytes=64)
             w_grouped_of[g] = w_grouped
-            cut = WV_VECTOR_COLS
             nc.vector.tensor_copy(
-                out=w_grouped[:, :cut, :].rearrange("p (c i) t -> p c t i", i=RUN),
-                in_=w_passes[g][:, :, :cut].rearrange("p t (c i) -> p c t i", i=RUN),
-            )
-            nc.scalar.copy(
-                out=w_grouped[:, cut:, :].rearrange("p (c i) t -> p c t i", i=RUN),
-                in_=w_passes[g][:, :, cut:].rearrange("p t (c i) -> p c t i", i=RUN),
+                out=w_grouped[:].rearrange("p (c i) t -> p c t i", i=RUN),
+                in_=w_passes[g][:].rearrange("p t (c i) -> p c t i", i=RUN),
             )
 
         def quantise_wv(g):
@@ -188,7 +177,7 @@ def tile_localselfattention_pa_k_kernel(tc, q, k_scaled, hidden_states, Wv, out)
                         )
                 dst = grouped_words[:, 2 * half : 2 * half + 2, :, :]
                 src = flipped[:].rearrange("p r u q -> p r q u")
-                if half == 0 or s < PASSES:
+                if half == 0 or s < PASSES or s % 4 == 3:
                     nc.scalar.copy(out=dst, in_=src)
                 else:
                     nc.vector.tensor_copy(out=dst, in_=src)
@@ -200,7 +189,7 @@ def tile_localselfattention_pa_k_kernel(tc, q, k_scaled, hidden_states, Wv, out)
             x_quantised[s] = (x_codes, x_scales)
 
         def project(s):
-            for r in range(PAIRS):
+            for r in ((2, 0, 3, 1) if s < PASSES else range(PAIRS)):
                 if s < PASSES:
                     tile_of_positions, g, bank = r, s, r
                 else:
@@ -269,8 +258,8 @@ def tile_localselfattention_pa_k_kernel(tc, q, k_scaled, hidden_states, Wv, out)
             j, h = tile_and_head(u)
             n, i = divmod(j, TILES)
             own = (i + 1) * P
-            queries = q_flipped[:, h, j * P : (j + 1) * P]
-            keys = k_flipped[:, h, n * CHUNK : n * CHUNK + own]
+            queries = qk_flipped[:, 0, h, j * P : (j + 1) * P]
+            keys = qk_flipped[:, 1, h, n * CHUNK : n * CHUNK + own]
             share = (h, h % 2, 0, 0)[i] if n == 0 else 0
             if share > 0:
                 s_own = s_own_of[u - 1][0]
@@ -290,8 +279,8 @@ def tile_localselfattention_pa_k_kernel(tc, q, k_scaled, hidden_states, Wv, out)
             s_prev = psum.tile([P, CHUNK], F32, tag=tag, name="s_prev")
             nc.tensor.matmul(
                 s_prev[:],
-                lhsT=q_flipped[:, h, j * P : (j + 1) * P],
-                rhs=k_flipped[:, h, (n - 1) * CHUNK : n * CHUNK],
+                lhsT=qk_flipped[:, 0, h, j * P : (j + 1) * P],
+                rhs=qk_flipped[:, 1, h, (n - 1) * CHUNK : n * CHUNK],
                 start=True,
                 stop=True,
             )
@@ -368,70 +357,63 @@ def tile_localselfattention_pa_k_kernel(tc, q, k_scaled, hidden_states, Wv, out)
                 nc.tensor.transpose(e_flip[:, b, :], words[:, b * P : (b + 1) * P], ident_f32[:])
             e_flip_of[u] = e_flip
 
+        def grouped_of(j):
+            return e_grouped[0 if j % TILES < 2 else 1 + j % 2]
+
         def regroup_e(u):
             j, h = tile_and_head(u)
             n, i = divmod(j, TILES)
             e_flip = e_flip_of[u]
+            words = grouped_of(j)[:].rearrange("p r h q t -> p (r h q t)").bitcast(F32).rearrange("p (r h q u) -> p r h q u", r=2, h=NH, u=2)
             own = place(u) // (2 * P)
+            if n > 0 and i >= 2:
+                nc.scalar.copy(out=words[:, :, h, :, :], in_=e_flip[:].rearrange("p (r u) q -> p r q u", r=2))
+                return
             blocks = i // 2 + 1
             nc.scalar.copy(
-                out=as_words(own_grouped[i])[:, h, :, :blocks],
+                out=words[:, 1, h, :, :blocks],
                 in_=e_flip[:, own : own + blocks, :].rearrange("p u q -> p q u"),
             )
             if n > 0:
-                if h == 0:
-                    prev_grouped_of[j] = stream.tile(
-                        [P, NH, P, PACK], BF16, tag="prev_grouped", name="prev_grouped", align_bytes=64
-                    )
-                nc.scalar.copy(out=as_words(prev_grouped_of[j])[:, h, :, :], in_=e_flip[:, :2, :].rearrange("p u q -> p q u"))
+                nc.scalar.copy(out=words[:, 0, h, :, :], in_=e_flip[:, :2, :].rearrange("p u q -> p q u"))
 
-        def as_words(grouped):
-            return grouped[:].rearrange("p h q t -> p (h q t)").bitcast(F32).rearrange("p (h q u) -> p h q u", h=NH, u=2)
+        def slots_of(j):
+            return slice(j, j + 1) if j < TILES else slice(2 * j - TILES, 2 * j - TILES + 2)
 
         def quantise_e(j):
-            n, i = divmod(j, TILES)
-            heads = slice(j * NH, (j + 1) * NH)
-            nc.vector.reciprocal(out=one_over_den[:, heads], in_=den[:, heads])
+            slots = slots_of(j)
+            first = 1 if j < TILES else 0
             nc.vector.quantize_mx(
-                out=e_codes[:, j, :].bitcast(FP8X4),
-                scales=e_scales[:, j, :],
-                in_=own_grouped[i][:].rearrange("p h q t -> p (h q t)"),
+                out=e_codes[:, slots, :].rearrange("p s c -> p (s c)").bitcast(FP8X4),
+                scales=e_scales[:, slots, :].rearrange("p s c -> p (s c)"),
+                in_=grouped_of(j)[:, first:, :, :, :].rearrange("p r h q t -> p (r h q t)"),
             )
-            if n > 0:
-                nc.vector.quantize_mx(
-                    out=e_codes[:, 2 * TILES + i, :].bitcast(FP8X4),
-                    scales=e_scales[:, 2 * TILES + i, :],
-                    in_=prev_grouped_of[j][:].rearrange("p h q t -> p (h q t)"),
-                )
+
+        def invert_den(n):
+            cols = slice(n * TILES * NH, (n + 1) * TILES * NH)
+            nc.vector.reciprocal(out=one_over_den[:, cols], in_=den[:, cols])
 
         def attend(j, heads, o):
-            n, i = divmod(j, TILES)
+            n = j // TILES
+            slots = slots_of(j)
             for h in heads:
                 cols = slice(h * DH, (h + 1) * DH)
-                nc.tensor.matmul_mx(
-                    out=o[:, cols],
-                    lhsT=e_codes[:, j, cols].bitcast(FP8X4),
-                    lhsT_scale=e_scales[:, j, cols],
-                    rhs=v_codes[:, n, cols].bitcast(FP8X4),
-                    rhs_scale=v_scales[:, n, cols],
-                    start=True,
-                    stop=(n == 0),
-                )
-                if n > 0:
+                for slot in range(slots.start, slots.stop):
+                    chunk = n - (slots.stop - 1 - slot)
                     nc.tensor.matmul_mx(
                         out=o[:, cols],
-                        lhsT=e_codes[:, 2 * TILES + i, cols].bitcast(FP8X4),
-                        lhsT_scale=e_scales[:, 2 * TILES + i, cols],
-                        rhs=v_codes[:, n - 1, cols].bitcast(FP8X4),
-                        rhs_scale=v_scales[:, n - 1, cols],
-                        start=False,
-                        stop=True,
+                        lhsT=e_codes[:, slot, cols].bitcast(FP8X4),
+                        lhsT_scale=e_scales[:, slot, cols],
+                        rhs=v_codes[:, chunk, cols].bitcast(FP8X4),
+                        rhs_scale=v_scales[:, chunk, cols],
+                        start=(slot == slots.start),
+                        stop=(slot == slots.stop - 1),
                     )
 
         def divide(j, heads, o, on_vector):
             cols = slice(heads[0] * DH, (heads[-1] + 1) * DH)
             recip = one_over_den[:, j * NH + heads[0] : j * NH + heads[-1] + 1]
-            o_sb = stream.tile([P, 2, DH], F32, tag="o_sb", bufs=6)
+            o_sb = stream.tile([P, len(heads), DH], F32, tag="o_sb%d" % len(heads), name="o_sb", bufs=(1 if len(heads) == NH else 5))
             if on_vector:
                 nc.vector.tensor_tensor(
                     out=o_sb[:],
@@ -461,15 +443,14 @@ def tile_localselfattention_pa_k_kernel(tc, q, k_scaled, hidden_states, Wv, out)
             j, h = tile_and_head(u)
             return j == 2 and h % 2 == 1 or j == TILES
 
-        qk_blocks_of = {
-            -1: ((0, 2), (1, 2)),
-            0: ((0, 3), (1, 3)),
-            6: ((0, 4),),
-            7: ((1, 4),),
-            8: ((0, 5),),
-            9: ((1, 5),),
-            14: ((1, 6), (1, 7)),
-            15: ((0, 7), (0, 6)),
+        qk_of = {
+            -1: (2, (0, 1)),
+            0: (3, (0, 1)),
+            6: (4, (0,)),
+            7: (4, (1,)),
+            14: (5, (0, 1)),
+            15: (7, (0, 1)),
+            16: (6, (0, 1)),
         }
 
         load_qk(0, 2)
@@ -502,7 +483,7 @@ def tile_localselfattention_pa_k_kernel(tc, q, k_scaled, hidden_states, Wv, out)
 
         for j in range(2):
             room = psum.tile([P, 2 * NH, P], BF16, tag="bank%d" % j, name="qk_flip")
-            flip_qk(((0, j), (1, j)), room, (nc.scalar.copy, nc.vector.tensor_copy))
+            flip_qk(j, (0, 1), room, (nc.scalar.copy, nc.vector.tensor_copy)[j])
         for u in range(NH):
             score_own(u)
 
@@ -523,20 +504,21 @@ def tile_localselfattention_pa_k_kernel(tc, q, k_scaled, hidden_states, Wv, out)
             for u in now:
                 if tile_and_head(u)[0] >= TILES and not second(u):
                     top_own(u)
+            if s >= PASSES and s % steps_of_a_tile == steps_of_a_tile - 1:
+                divide(s // steps_of_a_tile - TILES, range(NH), o, True)
             for u in before:
                 flip_e(u)
-            if s in qk_blocks_of:
+            if s in qk_of:
+                j, which = qk_of[s]
                 if s == -1:
                     room = psum.tile([P, 2 * NH, P], BF16, tag="bank2", name="qk_flip")
-                elif s == 0:
-                    room = psum.tile([P, 2 * NH, P], BF16, tag="e_flip", name="qk_flip")
                 elif s >= PASSES:
-                    room = psum.tile([P, 2 * NH, P], BF16, tag=("bank3", "bank1")[s - PASSES], name="qk_flip")
-                elif len(before) > 0:
-                    room = e_flip_of[before[0]][:].rearrange("p b q -> p (b q)").bitcast(BF16).rearrange("p (b q) -> p b q", q=P)
-                else:
+                    room = psum.tile([P, 2 * NH, P], BF16, tag="bank3", name="qk_flip")
+                elif len(which) == 2:
                     room = psum.tile([P, 2 * NH, P], BF16, tag="e_flip", name="qk_flip")
-                flip_qk(qk_blocks_of[s], room, (nc.scalar.copy, nc.vector.tensor_copy if s < 0 else nc.scalar.copy))
+                else:
+                    room = e_flip_of[before[0]][:].rearrange("p b q -> p (b q)").bitcast(BF16).rearrange("p (b q) -> p b q", q=P)
+                flip_qk(j, which, room, nc.vector.tensor_copy if s == -1 else nc.scalar.copy)
             for u in now:
                 if second(u):
                     score_own(u)
@@ -562,21 +544,19 @@ def tile_localselfattention_pa_k_kernel(tc, q, k_scaled, hidden_states, Wv, out)
                 regroup_v(0, 0)
                 regroup_v(0, 1)
             if s == PASSES + 1:
+                invert_den(0)
                 quantise_v(0, 0)
                 quantise_v(0, 1)
             if s >= 0:
                 project(s)
             if s == PASSES - 1:
                 round_v(2, nc.scalar.copy)
+                round_v(0, nc.vector.tensor_copy)
+                round_v(3, nc.scalar.copy)
                 round_v(1, nc.vector.tensor_copy)
-                round_v(0, nc.scalar.copy)
-                round_v(3, nc.vector.tensor_copy)
             if s >= PASSES and s % steps_of_a_tile == steps_of_a_tile - 2:
-                j = s // steps_of_a_tile - TILES
                 o = psum.tile([P, W], F32, tag="bank3", name="o")
-                attend(j, range(NH), o)
-                for half in HALVES:
-                    divide(j, half, o, False)
+                attend(s // steps_of_a_tile - TILES, range(NH), o)
             if PASSES <= s < STEPS - 1 and s % steps_of_a_tile == steps_of_a_tile - 1:
                 round_v(s // steps_of_a_tile, nc.scalar.copy)
             for u in after:
@@ -590,6 +570,7 @@ def tile_localselfattention_pa_k_kernel(tc, q, k_scaled, hidden_states, Wv, out)
         nc.vector.tensor_copy(out=v_rows_of[1][:, TILES - 1, half_cols[0]], in_=accs[last][:, half_cols[0]])
         regroup_v(1, 0)
         quantise_v(1, 0)
+        invert_den(1)
         acc = psum.tile([P, W], F32, tag="bank0", name="acc_last")
         for g in range(PASSES):
             multiply(acc, STEPS - PASSES // PAIRS + g // PAIRS, g % PAIRS, g, half_cols[1])

@@ -28,6 +28,7 @@ WORDS = K_PASS // 2
 LOAD_COLS = 2 * PAIRS * K_PASS
 RUN = 4
 MASKED = -1.0e9
+WV_VECTOR_COLS = 400
 WV_AHEAD = 5
 HALVES = ((0, 1), (2, 3))
 TILE_ORDER = (0, 1, 2, 3, 4, 5, 7, 6)
@@ -152,9 +153,14 @@ def tile_localselfattention_pa_k_kernel(tc, q, k_scaled, hidden_states, Wv, out)
         def regroup_wv(g):
             w_grouped = stream.tile([P, W, PACK], BF16, tag="w_grouped", align_bytes=64)
             w_grouped_of[g] = w_grouped
+            cut = WV_VECTOR_COLS
             nc.vector.tensor_copy(
-                out=w_grouped[:].rearrange("p (c i) t -> p c t i", i=RUN),
-                in_=w_passes[g][:].rearrange("p t (c i) -> p c t i", i=RUN),
+                out=w_grouped[:, :cut, :].rearrange("p (c i) t -> p c t i", i=RUN),
+                in_=w_passes[g][:, :, :cut].rearrange("p t (c i) -> p c t i", i=RUN),
+            )
+            nc.scalar.copy(
+                out=w_grouped[:, cut:, :].rearrange("p (c i) t -> p c t i", i=RUN),
+                in_=w_passes[g][:, :, cut:].rearrange("p t (c i) -> p c t i", i=RUN),
             )
 
         def quantise_wv(g):

@@ -28,7 +28,7 @@ WORDS = K_PASS // 2
 LOAD_COLS = 2 * PAIRS * K_PASS
 RUN = 4
 MASKED = -1.0e9
-WV_VECTOR_COLS = 400
+WV_VECTOR_COLS = 416
 WV_AHEAD = 5
 HALVES = ((0, 1), (2, 3))
 TILE_ORDER = (0, 1, 2, 3, 4, 5, 7, 6)
@@ -65,6 +65,8 @@ def tile_localselfattention_pa_k_kernel(tc, q, k_scaled, hidden_states, Wv, out)
             pattern=[[-1, P]],
             channel_multiplier=1,
         )
+        zeros = keep.tile([P, P], F32)
+        nc.gpsimd.memset(zeros[:], 0.0)
         later = keep.tile([P, P], BF16)
         nc.vector.tensor_copy(out=later[:], in_=later_f32[:])
 
@@ -78,7 +80,6 @@ def tile_localselfattention_pa_k_kernel(tc, q, k_scaled, hidden_states, Wv, out)
         den = keep.tile([P, 2 * TILES * NH], F32)
         one_over_den = keep.tile([P, 2 * TILES * NH], F32)
         e_grouped = [keep.tile([P, 2, NH, P, PACK], BF16, name="e_grouped%d" % b, align_bytes=64) for b in range(3)]
-        nc.gpsimd.memset(e_grouped[0][:, 1, :, :, :].rearrange("p h q t -> p (h q t)").bitcast(mybir.dt.int32), 0)
 
         x_blocks = {}
         w_passes = {}
@@ -183,7 +184,7 @@ def tile_localselfattention_pa_k_kernel(tc, q, k_scaled, hidden_states, Wv, out)
                         )
                 dst = grouped_words[:, 2 * half : 2 * half + 2, :, :]
                 src = flipped[:].rearrange("p r u q -> p r q u")
-                if half == 0 or s < PASSES or s % 4 == 3:
+                if half == 0 or s < PASSES or s % 4 in (0, 3):
                     nc.scalar.copy(out=dst, in_=src)
                 else:
                     nc.vector.tensor_copy(out=dst, in_=src)
@@ -248,17 +249,15 @@ def tile_localselfattention_pa_k_kernel(tc, q, k_scaled, hidden_states, Wv, out)
 
         def place(u):
             j, h = tile_and_head(u)
-            if j == 0:
-                return 2 * P * h
-            if j == 1:
-                return CHUNK + 2 * P * (h % 2)
+            if j < 2:
+                return 2 * P * (h % 2)
             if j == 2:
                 return CHUNK * (h % 2)
             return CHUNK
 
         def first_of_step(u):
             j, h = tile_and_head(u)
-            return (h if j == 0 else h % 2 if j < 3 else 0) == 0
+            return (h % 2 if j < 3 else 0) == 0
 
         def score_own(u):
             j, h = tile_and_head(u)
@@ -266,7 +265,7 @@ def tile_localselfattention_pa_k_kernel(tc, q, k_scaled, hidden_states, Wv, out)
             own = (i + 1) * P
             queries = qk_flipped[:, 0, h, j * P : (j + 1) * P]
             keys = qk_flipped[:, 1, h, n * CHUNK : n * CHUNK + own]
-            share = (h, h % 2, 0, 0)[i] if n == 0 else 0
+            share = h % 2 if j < 2 else 0
             if share > 0:
                 s_own = s_own_of[u - 1][0]
             else:
@@ -361,6 +360,8 @@ def tile_localselfattention_pa_k_kernel(tc, q, k_scaled, hidden_states, Wv, out)
             own = place(u) // (2 * P)
             for b in list(range(2 * n)) + list(range(own, own + i // 2 + 1)):
                 nc.tensor.transpose(e_flip[:, b, :], words[:, b * P : (b + 1) * P], ident_f32[:])
+            if i < 2 and first_of_step(u):
+                nc.tensor.transpose(e_flip[:, 2 + n, :], zeros[:], ident_f32[:])
             e_flip_of[u] = e_flip
 
         def grouped_of(j):
@@ -372,16 +373,11 @@ def tile_localselfattention_pa_k_kernel(tc, q, k_scaled, hidden_states, Wv, out)
             e_flip = e_flip_of[u]
             words = grouped_of(j)[:].rearrange("p r h q t -> p (r h q t)").bitcast(F32).rearrange("p (r h q u) -> p r h q u", r=2, h=NH, u=2)
             own = place(u) // (2 * P)
-            if n > 0 and i >= 2:
+            if n > 0:
                 nc.scalar.copy(out=words[:, :, h, :, :], in_=e_flip[:].rearrange("p (r u) q -> p r q u", r=2))
                 return
-            blocks = i // 2 + 1
-            nc.scalar.copy(
-                out=words[:, 1, h, :, :blocks],
-                in_=e_flip[:, own : own + blocks, :].rearrange("p u q -> p q u"),
-            )
-            if n > 0:
-                nc.scalar.copy(out=words[:, 0, h, :, :], in_=e_flip[:, :2, :].rearrange("p u q -> p q u"))
+            first = e_flip[:, own : own + 2, :] if i >= 2 else e_flip[:, own : 3 : 2 - own, :]
+            nc.scalar.copy(out=words[:, 1, h, :, :], in_=first.rearrange("p u q -> p q u"))
 
         def slots_of(j):
             return slice(j, j + 1) if j < TILES else slice(2 * j - TILES, 2 * j - TILES + 2)
@@ -416,13 +412,12 @@ def tile_localselfattention_pa_k_kernel(tc, q, k_scaled, hidden_states, Wv, out)
                         stop=(slot == slots.stop - 1),
                     )
 
-        def divide(j, heads, o, on_vector):
+        def divide(j, heads, o, o_sb, on_vector):
             cols = slice(heads[0] * DH, (heads[-1] + 1) * DH)
             recip = one_over_den[:, j * NH + heads[0] : j * NH + heads[-1] + 1]
-            o_sb = stream.tile([P, len(heads), DH], F32, tag="o_sb%d" % len(heads), name="o_sb", bufs=(1 if len(heads) == NH else 5))
             if on_vector:
                 nc.vector.tensor_tensor(
-                    out=o_sb[:],
+                    out=o_sb,
                     in0=o[:, cols].rearrange("p (h d) -> p h d", d=DH),
                     in1=recip.unsqueeze(2).to_broadcast([P, len(heads), DH]),
                     op=ALU.mult,
@@ -432,15 +427,13 @@ def tile_localselfattention_pa_k_kernel(tc, q, k_scaled, hidden_states, Wv, out)
                     nc.scalar.activation(
                         out=o_sb[:, b, :], in_=o[:, h * DH : (h + 1) * DH], func=ACT.Copy, scale=recip[:, b : b + 1]
                     )
-            nc.sync.dma_start(out=out_rows[j * P : (j + 1) * P, cols], in_=o_sb[:].rearrange("p h d -> p (h d)"))
+            nc.sync.dma_start(out=out_rows[j * P : (j + 1) * P, cols], in_=o_sb.rearrange("p h d -> p (h d)"))
 
         def softmaxes_of(s):
-            if s == -1:
-                return (0, 1, 2, 3)
-            if 0 <= s <= 3:
-                return (2 * s + 4, 2 * s + 5)
-            if 4 <= s <= 11:
-                return (s + 8,)
+            if -1 <= s <= 4:
+                return (2 * s + 2, 2 * s + 3)
+            if 5 <= s <= 12:
+                return (s + 7,)
             if PASSES <= s < PASSES + 12:
                 return (s + 4,)
             return ()
@@ -452,16 +445,16 @@ def tile_localselfattention_pa_k_kernel(tc, q, k_scaled, hidden_states, Wv, out)
         qk_of = {
             -1: (2, (0, 1)),
             0: (3, (0, 1)),
-            6: (4, (0,)),
-            7: (4, (1,)),
-            14: (5, (0, 1)),
-            15: (7, (0, 1)),
-            16: (6, (0, 1)),
+            7: (4, (0,)),
+            8: (4, (1,)),
+            15: (5, (0, 1)),
+            16: (7, (0, 1)),
+            17: (6, (0, 1)),
         }
 
+        load_wv(0)
         load_qk(0, 2)
         load_hidden(0, 1)
-        load_wv(0)
         load_qk(2, 4)
         for g in range(1, 4):
             load_hidden(g, 1)
@@ -487,10 +480,12 @@ def tile_localselfattention_pa_k_kernel(tc, q, k_scaled, hidden_states, Wv, out)
             23: [lambda: load_half_tile(30)],
         }
 
+        regroup_wv(0)
         for j in range(2):
             room = psum.tile([P, 2 * NH, P], BF16, tag="bank%d" % j, name="qk_flip")
             flip_qk(j, (0, 1), room, (nc.scalar.copy, nc.vector.tensor_copy)[j])
-        for u in range(NH):
+        quantise_wv(0)
+        for u in range(2):
             score_own(u)
 
         steps_of_a_tile = PASSES // PAIRS
@@ -505,13 +500,14 @@ def tile_localselfattention_pa_k_kernel(tc, q, k_scaled, hidden_states, Wv, out)
                     top_prev(u)
                 elif not second(u):
                     top_own(u)
-            if 0 <= s + 1 < STEPS:
-                flip_hidden(s + 1)
+            if s <= 8 or s + 2 < STEPS:
+                flip_hidden(s + 1 if s <= 8 else s + 2)
             for u in now:
                 if tile_and_head(u)[0] >= TILES and not second(u):
                     top_own(u)
             if s >= PASSES and s % steps_of_a_tile == steps_of_a_tile - 1:
-                divide(s // steps_of_a_tile - TILES, range(NH), o, True)
+                o_sb = stream.tile([P, NH, DH], F32, tag="o_sb", bufs=1)
+                divide(s // steps_of_a_tile - TILES, range(NH), o, o_sb[:], True)
             for u in before:
                 flip_e(u)
             if s in qk_of:
@@ -528,7 +524,7 @@ def tile_localselfattention_pa_k_kernel(tc, q, k_scaled, hidden_states, Wv, out)
             for u in now:
                 if second(u):
                     score_own(u)
-            if 0 <= s + 1 < PASSES:
+            if 0 < s + 1 < PASSES:
                 regroup_wv(s + 1)
             for u in before:
                 regroup_e(u)
@@ -541,7 +537,7 @@ def tile_localselfattention_pa_k_kernel(tc, q, k_scaled, hidden_states, Wv, out)
                 if second(u):
                     top_own(u)
                     exponential(u)
-            if 0 <= s + 1 < PASSES:
+            if 0 < s + 1 < PASSES:
                 quantise_wv(s + 1)
             for u in before:
                 if u % NH == NH - 1:
@@ -555,11 +551,13 @@ def tile_localselfattention_pa_k_kernel(tc, q, k_scaled, hidden_states, Wv, out)
                 quantise_v(0, 1)
             if s >= 0:
                 project(s)
+            if s == 8:
+                flip_hidden(s + 2)
             if s == PASSES - 1:
                 round_v(2, nc.scalar.copy)
-                round_v(0, nc.vector.tensor_copy)
+                round_v(0, nc.scalar.copy)
                 round_v(3, nc.scalar.copy)
-                round_v(1, nc.vector.tensor_copy)
+                round_v(1, nc.scalar.copy)
             if s >= PASSES and s % steps_of_a_tile == steps_of_a_tile - 2:
                 o = psum.tile([P, W], F32, tag="bank3", name="o")
                 attend(s // steps_of_a_tile - TILES, range(NH), o)
@@ -583,8 +581,10 @@ def tile_localselfattention_pa_k_kernel(tc, q, k_scaled, hidden_states, Wv, out)
         nc.vector.tensor_copy(out=v_rows_of[1][:, TILES - 1, half_cols[1]], in_=acc[:, half_cols[1]])
         regroup_v(1, 1)
         quantise_v(1, 1)
+        o_raw = stream.tile([P, LOAD_COLS], BF16, tag="x_raw", name="x_raw", bufs=4)
+        o_parts = o_raw[:].bitcast(F32).rearrange("p (n h d) -> p n h d", h=2, d=DH)
         for half, tags in enumerate((("bank2", "bank3", "s_own", "e_flip"), ("bank1", "x_flip", "x_flip", "bank0"))):
-            for j, tag in zip(TILE_ORDER[TILES:], tags):
+            for n, (j, tag) in enumerate(zip(TILE_ORDER[TILES:], tags)):
                 o = psum.tile([P, W], F32, tag=tag, name="o", bufs=(2 if tag == "x_flip" else 1))
                 attend(j, HALVES[half], o)
-                divide(j, HALVES[half], o, half == 1 and j % 2 == 0)
+                divide(j, HALVES[half], o, o_parts[:, half * TILES + n, :, :], half == 1 and j % 2 == 0)

@@ -28,7 +28,8 @@ WORDS = K_PASS // 2
 LOAD_COLS = 2 * PAIRS * K_PASS
 RUN = 4
 MASKED = -1.0e9
-WV_VECTOR_COLS = 416
+WV_VECTOR_COLS = 432
+LATER_QUANTISED = {17: 4, 20: 3, 24: 2, STEPS - 2: 6}
 WV_AHEAD = 5
 HALVES = ((0, 1), (2, 3))
 TILE_ORDER = (0, 1, 2, 3, 4, 5, 7, 6)
@@ -507,7 +508,7 @@ def tile_localselfattention_pa_k_kernel(tc, q, k_scaled, hidden_states, Wv, out)
                     top_own(u)
             if s >= PASSES and s % steps_of_a_tile == steps_of_a_tile - 1:
                 o_sb = stream.tile([P, NH, DH], F32, tag="o_sb", bufs=1)
-                divide(s // steps_of_a_tile - TILES, range(NH), o, o_sb[:], True)
+                divide(s // steps_of_a_tile - TILES, range(NH), o, o_sb[:], s < STEPS - 1)
             for u in before:
                 flip_e(u)
             if s in qk_of:
@@ -540,8 +541,10 @@ def tile_localselfattention_pa_k_kernel(tc, q, k_scaled, hidden_states, Wv, out)
             if 0 < s + 1 < PASSES:
                 quantise_wv(s + 1)
             for u in before:
-                if u % NH == NH - 1:
+                if u % NH == NH - 1 and tile_and_head(u)[0] not in (2, 3, 4, 6):
                     quantise_e(tile_and_head(u)[0])
+            if s in LATER_QUANTISED:
+                quantise_e(LATER_QUANTISED[s])
             if s == PASSES:
                 regroup_v(0, 0)
                 regroup_v(0, 1)

@@ -26,7 +26,7 @@ PAIRS = 4
 STEPS = 2 * TILES * PASSES // PAIRS
 WORDS = K_PASS // 2
 LOAD_COLS = 2 * PAIRS * K_PASS
-RUN = 4
+RUN = 8
 MASKED = -1.0e9
 WV_VECTOR_COLS = 432
 LATER_QUANTISED = {17: 4, 20: 3, 24: 2, STEPS - 2: 6}

@@ -28,8 +28,8 @@ WORDS = K_PASS // 2
 LOAD_COLS = 2 * PAIRS * K_PASS
 RUN = 8
 MASKED = -1.0e9
-WV_VECTOR_COLS = 432
-LATER_QUANTISED = {17: 4, 20: 3, 24: 2, STEPS - 2: 6}
+WV_VECTOR_COLS = 448
+LATER_QUANTISED = {15: 4, 20: 3, 19: 2, 30: 6}
 WV_AHEAD = 5
 HALVES = ((0, 1), (2, 3))
 TILE_ORDER = (0, 1, 2, 3, 4, 5, 7, 6)
@@ -380,6 +380,11 @@ def tile_localselfattention_pa_k_kernel(tc, q, k_scaled, hidden_states, Wv, out)
             first = e_flip[:, own : own + 2, :] if i >= 2 else e_flip[:, own : 3 : 2 - own, :]
             nc.scalar.copy(out=words[:, 1, h, :, :], in_=first.rearrange("p u q -> p q u"))
 
+        def regroup_e_pair(u):
+            j, h = tile_and_head(u)
+            words = grouped_of(j)[:, 1, h : h + 2, :, :].rearrange("p h q t -> p (h q t)").bitcast(F32).rearrange("p (h q u) -> p h q u", h=2, u=2)
+            nc.scalar.copy(out=words, in_=e_flip_of[u][:].rearrange("p (h u) q -> p h q u", u=2))
+
         def slots_of(j):
             return slice(j, j + 1) if j < TILES else slice(2 * j - TILES, 2 * j - TILES + 2)
 
@@ -506,9 +511,9 @@ def tile_localselfattention_pa_k_kernel(tc, q, k_scaled, hidden_states, Wv, out)
             for u in now:
                 if tile_and_head(u)[0] >= TILES and not second(u):
                     top_own(u)
-            if s >= PASSES and s % steps_of_a_tile == steps_of_a_tile - 1:
+            if s in (23, 26, 29, 31):
                 o_sb = stream.tile([P, NH, DH], F32, tag="o_sb", bufs=1)
-                divide(s // steps_of_a_tile - TILES, range(NH), o, o_sb[:], s < STEPS - 1)
+                divide((23, 26, 29, 31).index(s), range(NH), o, o_sb[:], s < 31)
             for u in before:
                 flip_e(u)
             if s in qk_of:
@@ -521,14 +526,17 @@ def tile_localselfattention_pa_k_kernel(tc, q, k_scaled, hidden_states, Wv, out)
                     room = psum.tile([P, 2 * NH, P], BF16, tag="e_flip", name="qk_flip")
                 else:
                     room = e_flip_of[before[0]][:].rearrange("p b q -> p (b q)").bitcast(BF16).rearrange("p (b q) -> p b q", q=P)
-                flip_qk(j, which, room, nc.vector.tensor_copy if s == -1 else nc.scalar.copy)
+                flip_qk(j, which, room, nc.vector.tensor_copy if s in (-1, 15,) else nc.scalar.copy)
             for u in now:
                 if second(u):
                     score_own(u)
             if 0 < s + 1 < PASSES:
                 regroup_wv(s + 1)
-            for u in before:
-                regroup_e(u)
+            if len(before) == 2 and tile_and_head(before[0])[0] == 2:
+                regroup_e_pair(before[0])
+            else:
+                for u in before:
+                    regroup_e(u)
             for u in now:
                 if not second(u):
                     exponential(u)
@@ -545,10 +553,10 @@ def tile_localselfattention_pa_k_kernel(tc, q, k_scaled, hidden_states, Wv, out)
                     quantise_e(tile_and_head(u)[0])
             if s in LATER_QUANTISED:
                 quantise_e(LATER_QUANTISED[s])
-            if s == PASSES:
+            if s == 16:
                 regroup_v(0, 0)
                 regroup_v(0, 1)
-            if s == PASSES + 1:
+            if s == 17:
                 invert_den(0)
                 quantise_v(0, 0)
                 quantise_v(0, 1)
@@ -561,9 +569,9 @@ def tile_localselfattention_pa_k_kernel(tc, q, k_scaled, hidden_states, Wv, out)
                 round_v(0, nc.scalar.copy)
                 round_v(3, nc.scalar.copy)
                 round_v(1, nc.scalar.copy)
-            if s >= PASSES and s % steps_of_a_tile == steps_of_a_tile - 2:
+            if s >= PASSES and s in (22, 25, 28, 30):
                 o = psum.tile([P, W], F32, tag="bank3", name="o")
-                attend(s // steps_of_a_tile - TILES, range(NH), o)
+                attend((22, 25, 28, 30).index(s), range(NH), o)
             if PASSES <= s < STEPS - 1 and s % steps_of_a_tile == steps_of_a_tile - 1:
                 round_v(s // steps_of_a_tile, nc.scalar.copy)
             for u in after:
@@ -590,4 +598,4 @@ def tile_localselfattention_pa_k_kernel(tc, q, k_scaled, hidden_states, Wv, out)
             for n, (j, tag) in enumerate(zip(TILE_ORDER[TILES:], tags)):
                 o = psum.tile([P, W], F32, tag=tag, name="o", bufs=(2 if tag == "x_flip" else 1))
                 attend(j, HALVES[half], o)
-                divide(j, HALVES[half], o, o_parts[:, half * TILES + n, :, :], half == 1 and j % 2 == 0)
+                divide(j, HALVES[half], o, o_parts[:, half * TILES + n, :, :], n == 3 if half == 0 else n % 2 == 1)

@@ -72,12 +72,12 @@ def tile_localselfattention_pa_k_kernel(tc, q, k_scaled, hidden_states, Wv, out)
         nc.vector.tensor_copy(out=later[:], in_=later_f32[:])
 
         qk_flipped = keep.tile([P, 2, NH, S], BF16)
-        wv_codes = keep.tile([P, PASSES, W], U32, align_bytes=64)
-        wv_scales = keep.tile([P, PASSES, W], U8, align_bytes=64)
-        v_codes = keep.tile([P, 2, W], U32, align_bytes=64)
-        v_scales = keep.tile([P, 2, W], U8, align_bytes=64)
-        e_codes = keep.tile([P, 3 * TILES, W], U32, align_bytes=64)
-        e_scales = keep.tile([P, 3 * TILES, W], U8, align_bytes=64)
+        wv_codes = keep.tile([P, PASSES, W], U32, align_bytes=256)
+        wv_scales = keep.tile([P, PASSES, W], U8, align_bytes=256)
+        v_codes = keep.tile([P, 2, W], U32, align_bytes=256)
+        v_scales = keep.tile([P, 2, W], U8, align_bytes=256)
+        e_codes = keep.tile([P, 3 * TILES, W], U32, align_bytes=256)
+        e_scales = keep.tile([P, 3 * TILES, W], U8, align_bytes=256)
         den = keep.tile([P, 2 * TILES * NH], F32)
         one_over_den = keep.tile([P, 2 * TILES * NH], F32)
         e_grouped = [keep.tile([P, 2, NH, P, PACK], BF16, name="e_grouped%d" % b, align_bytes=64) for b in range(3)]
@@ -191,8 +191,8 @@ def tile_localselfattention_pa_k_kernel(tc, q, k_scaled, hidden_states, Wv, out)
                     nc.vector.tensor_copy(out=dst, in_=src)
 
         def quantise_hidden(s):
-            x_codes = stream.tile([P, PAIRS * P], U32, tag="x_codes", bufs=5, align_bytes=64)
-            x_scales = stream.tile([P, PAIRS * P], U8, tag="x_scales", bufs=5, align_bytes=64)
+            x_codes = stream.tile([P, PAIRS * P], U32, tag="x_codes", bufs=5, align_bytes=256)
+            x_scales = stream.tile([P, PAIRS * P], U8, tag="x_scales", bufs=5, align_bytes=256)
             nc.vector.quantize_mx(out=x_codes[:].bitcast(FP8X4), scales=x_scales[:], in_=x_grouped_of[s][:])
             x_quantised[s] = (x_codes, x_scales)
 

@@ -353,7 +353,8 @@ def tile_localselfattention_pa_k_kernel(tc, q, k_scaled, hidden_states, Wv, out)
 
         def flip_e(u):
             n, i = divmod(tile_and_head(u)[0], TILES)
-            if first_of_step(u):
+            j, h = tile_and_head(u)
+            if first_of_step(u) and (i > 1 or h == 0):
                 e_flip = psum.tile([P, TILES, P], F32, tag="e_flip", name="e_flip")
             else:
                 e_flip = e_flip_of[u - 1]
@@ -361,7 +362,7 @@ def tile_localselfattention_pa_k_kernel(tc, q, k_scaled, hidden_states, Wv, out)
             own = place(u) // (2 * P)
             for b in list(range(2 * n)) + list(range(own, own + i // 2 + 1)):
                 nc.tensor.transpose(e_flip[:, b, :], words[:, b * P : (b + 1) * P], ident_f32[:])
-            if i < 2 and first_of_step(u):
+            if i < 2 and h == 0:
                 nc.tensor.transpose(e_flip[:, 2 + n, :], zeros[:], ident_f32[:])
             e_flip_of[u] = e_flip
 
@@ -540,12 +541,12 @@ def tile_localselfattention_pa_k_kernel(tc, q, k_scaled, hidden_states, Wv, out)
             for u in now:
                 if not second(u):
                     exponential(u)
-            if 0 <= s + 1 < STEPS:
-                quantise_hidden(s + 1)
             for u in now:
                 if second(u):
                     top_own(u)
                     exponential(u)
+            if 0 <= s + 1 < STEPS:
+                quantise_hidden(s + 1)
             if 0 < s + 1 < PASSES:
                 quantise_wv(s + 1)
             for u in before:
@@ -585,11 +586,11 @@ def tile_localselfattention_pa_k_kernel(tc, q, k_scaled, hidden_states, Wv, out)
         nc.vector.tensor_copy(out=v_rows_of[1][:, TILES - 1, half_cols[0]], in_=accs[last][:, half_cols[0]])
         regroup_v(1, 0)
         quantise_v(1, 0)
-        invert_den(1)
         acc = psum.tile([P, W], F32, tag="bank0", name="acc_last")
         for g in range(PASSES):
             multiply(acc, STEPS - PASSES // PAIRS + g // PAIRS, g % PAIRS, g, half_cols[1])
         nc.vector.tensor_copy(out=v_rows_of[1][:, TILES - 1, half_cols[1]], in_=acc[:, half_cols[1]])
+        invert_den(1)
         regroup_v(1, 1)
         quantise_v(1, 1)
         o_raw = stream.tile([P, LOAD_COLS], BF16, tag="x_raw", name="x_raw", bufs=4)

from contextlib import ExitStack

import concourse.mybir as mybir
from concourse.masks import make_identity

BF16 = mybir.dt.bfloat16
F32 = mybir.dt.float32
U32 = mybir.dt.uint32
U8 = mybir.dt.uint8
FP8X4 = mybir.dt.float8_e4m3fn_x4
ALU = mybir.AluOpType
ACT = mybir.ActivationFunctionType

P = 128
PACK = 4
K_PASS = P * PACK
S = 1024
HID = 8192
NH = 4
DH = 128
W = NH * DH
CHUNK = 512
TILES = CHUNK // P
PASSES = HID // K_PASS
PAIRS = 4
STEPS = 2 * TILES * PASSES // PAIRS
WORDS = K_PASS // 2
LOAD_COLS = 2 * PAIRS * K_PASS
RUN = 8
MASKED = -1.0e9
WV_VECTOR_COLS = 448
LATER_QUANTISED = {15: 4, 20: 3, 19: 2, 30: 6}
WV_AHEAD = 5
HALVES = ((0, 1), (2, 3))
TILE_ORDER = (0, 1, 2, 3, 4, 5, 7, 6)


FLOPS = 2 * S * HID * W + 2 * 2 * NH * 3 * CHUNK * CHUNK * DH


def tile_localselfattention_pa_k_kernel(tc, q, k_scaled, hidden_states, Wv, out):
    nc = tc.nc
    q_rows = q.flatten_outer_dims()
    k_rows = k_scaled.flatten_outer_dims()
    x_rows = hidden_states.flatten_outer_dims()
    out_rows = out.flatten_outer_dims()

    with ExitStack() as ctx:
        ctx.enter_context(tc.manual_schedule())
        keep = ctx.enter_context(tc.tile_pool(name="keep", bufs=1))
        stream = ctx.enter_context(tc.tile_pool(name="stream", bufs=2))
        psum = ctx.enter_context(tc.psum_pool(name="psum", bufs=1))

        ident_bf = keep.tile([P, P], BF16)
        make_identity(nc, ident_bf[:])
        ident_f32 = keep.tile([P, P], F32)
        make_identity(nc, ident_f32[:])
        later_f32 = keep.tile([P, P], F32)
        nc.gpsimd.memset(later_f32[:], 0.0)
        nc.gpsimd.affine_select(
            out=later_f32[:],
            in_=later_f32[:],
            compare_op=ALU.is_ge,
            fill=MASKED,
            base=0,
            pattern=[[-1, P]],
            channel_multiplier=1,
        )
        zeros = keep.tile([P, P], F32)
        nc.gpsimd.memset(zeros[:], 0.0)
        later = keep.tile([P, P], BF16)
        nc.vector.tensor_copy(out=later[:], in_=later_f32[:])

        qk_flipped = keep.tile([P, 2, NH, S], BF16)
        wv_codes = keep.tile([P, PASSES, W], U32, align_bytes=256)
        wv_scales = keep.tile([P, PASSES, W], U8, align_bytes=256)
        v_codes = keep.tile([P, 2, W], U32, align_bytes=256)
        v_scales = keep.tile([P, 2, W], U8, align_bytes=256)
        e_codes = keep.tile([P, 3 * TILES, W], U32, align_bytes=256)
        e_scales = keep.tile([P, 3 * TILES, W], U8, align_bytes=256)
        den = keep.tile([P, 2 * TILES * NH], F32)
        one_over_den = keep.tile([P, 2 * TILES * NH], F32)
        e_grouped = [keep.tile([P, 2, NH, P, PACK], BF16, name="e_grouped%d" % b, align_bytes=64) for b in range(3)]

        x_blocks = {}
        w_passes = {}
        x_grouped_of = {}
        w_grouped_of = {}
        x_quantised = {}
        accs = {}
        s_own_of = {}
        s_prev_of = {}
        scores_of = {}
        e_of = {}
        e_flip_of = {}
        v_rows_of = {}
        v_grouped_of = {}

        qk_raw = keep.tile([P, 2, TILES, W], BF16)

        def load_qk(first, last):
            for o, rows in enumerate((q_rows, k_rows)):
                nc.sync.dma_start(
                    out=qk_raw[:, o, first % TILES : (last - 1) % TILES + 1, :],
                    in_=rows[first * P : last * P, :].rearrange("(t p) w -> p t w", p=P),
                )

        def load_hidden(g, count):
            x_raw = stream.tile([P, LOAD_COLS], BF16, tag="x_raw", name="x_raw", bufs=4)
            used = x_raw[:, : TILES * count * K_PASS].rearrange("p (t k) -> p t k", t=TILES)
            for u in range(2):
                nc.sync.dma_start(
                    out=used[:, 2 * u : 2 * u + 2, :],
                    in_=x_rows[2 * P * u : 2 * P * (u + 1), g * K_PASS : (g + count) * K_PASS].rearrange("(p e) k -> p e k", e=2),
                )
            for local in range(count):
                x_blocks[g + local] = [
                    used[:, t, local * K_PASS : (local + 1) * K_PASS].bitcast(F32) for t in range(TILES)
                ]

        def load_wv(g):
            w_raw = stream.tile([P, PACK, W], BF16, tag="w_raw", name="w_raw", bufs=WV_AHEAD)
            nc.sync.dma_start(
                out=w_raw[:].rearrange("p (s e) c -> p s (e c)", e=2),
                in_=Wv[g * K_PASS : (g + 1) * K_PASS, :].rearrange("(s p e) c -> p s (e c)", p=P, e=2),
            )
            w_passes[g] = w_raw

        def load_half_tile(s):
            x_raw = stream.tile([P, LOAD_COLS], BF16, tag="x_raw", name="x_raw", bufs=4)
            tile_of_positions, first_pass = divmod(s * PAIRS, PASSES)
            first_row = tile_of_positions // 2 * 2 * P
            first_col = first_pass * K_PASS
            nc.sync.dma_start(
                out=x_raw[:],
                in_=x_rows[first_row : first_row + 2 * P, first_col : first_col + LOAD_COLS].rearrange("(p e) k -> p e k", e=2)[
                    :, tile_of_positions % 2, :
                ],
            )
            for local in range(2):
                first = local * PAIRS * K_PASS
                x_blocks[s + local] = [
                    x_raw[:, first + r * K_PASS : first + (r + 1) * K_PASS].bitcast(F32) for r in range(PAIRS)
                ]

        def flip_qk(j, which, flipped, copy):
            for b, o in enumerate(which):
                for h in range(NH):
                    nc.tensor.transpose(flipped[:, b * NH + h, :], qk_raw[:, o, j % TILES, h * DH : (h + 1) * DH], ident_bf[:])
            copy(
                out=qk_flipped[:, which[0] : which[-1] + 1, :, j * P : (j + 1) * P],
                in_=flipped[:, : len(which) * NH, :].rearrange("p (o h) q -> p o h q", h=NH),
            )

        def regroup_wv(g):
            w_grouped = stream.tile([P, W, PACK], BF16, tag="w_grouped", align_bytes=64)
            w_grouped_of[g] = w_grouped
            cut = WV_VECTOR_COLS
            nc.vector.tensor_copy(
                out=w_grouped[:, :cut, :].rearrange("p (c i) t -> p c t i", i=RUN),
                in_=w_passes[g][:, :, :cut].rearrange("p t (c i) -> p c t i", i=RUN),
            )
            nc.scalar.copy(
                out=w_grouped[:, cut:, :].rearrange("p (c i) t -> p c t i", i=RUN),
                in_=w_passes[g][:, :, cut:].rearrange("p t (c i) -> p c t i", i=RUN),
            )

        def quantise_wv(g):
            nc.vector.quantize_mx(
                out=wv_codes[:, g, :].bitcast(FP8X4),
                scales=wv_scales[:, g, :],
                in_=w_grouped_of[g][:].rearrange("p c t -> p (c t)"),
            )

        def flip_hidden(s):
            x_grouped = stream.tile([P, PAIRS * P * PACK], BF16, tag="x_grouped", align_bytes=64)
            x_grouped_of[s] = x_grouped
            grouped_words = x_grouped[:].bitcast(F32).rearrange("p (r q u) -> p r q u", r=PAIRS, u=2)
            for half in range(2):
                flipped = psum.tile([P, 2, 2, P], F32, tag="x_flip", bufs=2)
                for r in range(2):
                    for u in range(2):
                        nc.tensor.transpose(
                            flipped[:, r, u, :], x_blocks[s][2 * half + r][:, u * P : (u + 1) * P], ident_f32[:]
                        )
                dst = grouped_words[:, 2 * half : 2 * half + 2, :, :]
                src = flipped[:].rearrange("p r u q -> p r q u")
                if half == 0 or s < PASSES or s % 4 in (0, 3):
                    nc.scalar.copy(out=dst, in_=src)
                else:
                    nc.vector.tensor_copy(out=dst, in_=src)

        def quantise_hidden(s):
            x_codes = stream.tile([P, PAIRS * P], U32, tag="x_codes", bufs=5, align_bytes=256)
            x_scales = stream.tile([P, PAIRS * P], U8, tag="x_scales", bufs=5, align_bytes=256)
            nc.vector.quantize_mx(out=x_codes[:].bitcast(FP8X4), scales=x_scales[:], in_=x_grouped_of[s][:])
            x_quantised[s] = (x_codes, x_scales)

        def project(s):
            for r in ((2, 0, 3, 1) if s < PASSES else range(PAIRS)):
                if s < PASSES:
                    tile_of_positions, g, bank = r, s, r
                else:
                    tile_of_positions, g = divmod(s * PAIRS + r, PASSES)
                    bank = tile_of_positions % 2
                if g == 0:
                    accs[tile_of_positions] = psum.tile(
                        [P, W], F32, tag="bank%d" % bank, name="acc%d" % tile_of_positions
                    )
                last = tile_of_positions == 2 * TILES - 1
                multiply(accs[tile_of_positions], s, r, g, slice(0, W // 2 if last else W))

        def multiply(acc, s, r, g, out_cols):
            x_codes, x_scales = x_quantised[s]
            cols = slice(r * P, (r + 1) * P)
            nc.tensor.matmul_mx(
                out=acc[:, out_cols],
                lhsT=x_codes[:, cols].bitcast(FP8X4),
                lhsT_scale=x_scales[:, cols],
                rhs=wv_codes[:, g, out_cols].bitcast(FP8X4),
                rhs_scale=wv_scales[:, g, out_cols],
                start=(g == 0),
                stop=(g == PASSES - 1),
            )

        def round_v(tile_of_positions, copy):
            n, t = divmod(tile_of_positions, TILES)
            copy(out=v_rows_of[n][:, t, :], in_=accs[tile_of_positions][:])

        def regroup_v(n, half):
            if half == 0:
                v_grouped_of[n] = stream.tile([P, W, PACK], BF16, tag="v_grouped", name="v_grouped", bufs=1, align_bytes=64)
            cols = slice(half * W // 2, (half + 1) * W // 2)
            nc.vector.tensor_copy(
                out=v_grouped_of[n][:, cols, :].rearrange("p (c i) t -> p c t i", i=RUN),
                in_=v_rows_of[n][:, :, cols].rearrange("p t (c i) -> p c t i", i=RUN),
            )

        def quantise_v(n, half):
            cols = slice(half * W // 2, (half + 1) * W // 2)
            nc.vector.quantize_mx(
                out=v_codes[:, n, cols].bitcast(FP8X4),
                scales=v_scales[:, n, cols],
                in_=v_grouped_of[n][:, cols, :].rearrange("p c t -> p (c t)"),
            )

        def tile_and_head(u):
            order, h = divmod(u, NH)
            return TILE_ORDER[order], h

        def place(u):
            j, h = tile_and_head(u)
            if j < 2:
                return 2 * P * (h % 2)
            if j == 2:
                return CHUNK * (h % 2)
            return CHUNK

        def first_of_step(u):
            j, h = tile_and_head(u)
            return (h % 2 if j < 3 else 0) == 0

        def score_own(u):
            j, h = tile_and_head(u)
            n, i = divmod(j, TILES)
            own = (i + 1) * P
            queries = qk_flipped[:, 0, h, j * P : (j + 1) * P]
            keys = qk_flipped[:, 1, h, n * CHUNK : n * CHUNK + own]
            share = h % 2 if j < 2 else 0
            if share > 0:
                s_own = s_own_of[u - 1][0]
            else:
                s_own = psum.tile([P, CHUNK], F32, tag="s_own", name="s_own")
            first = share * own
            s_own_of[u] = (s_own, first)
            if i > 0:
                nc.tensor.matmul(s_own[:, first : first + i * P], lhsT=queries, rhs=keys[:, : i * P], start=True, stop=True)
            diagonal = s_own[:, first + i * P : first + own]
            nc.tensor.matmul(diagonal, lhsT=ident_bf[:], rhs=later[:], start=True, stop=False)
            nc.tensor.matmul(diagonal, lhsT=queries, rhs=keys[:, i * P : own], start=False, stop=True)

        def score_prev(u, tag):
            j, h = tile_and_head(u)
            n = j // TILES
            s_prev = psum.tile([P, CHUNK], F32, tag=tag, name="s_prev")
            nc.tensor.matmul(
                s_prev[:],
                lhsT=qk_flipped[:, 0, h, j * P : (j + 1) * P],
                rhs=qk_flipped[:, 1, h, (n - 1) * CHUNK : n * CHUNK],
                start=True,
                stop=True,
            )
            s_prev_of[u] = s_prev

        def scores_tile(u):
            if u not in scores_of:
                if first_of_step(u):
                    minus_scores = stream.tile([P, 2 * CHUNK], F32, tag="minus_scores", name="minus_scores")
                else:
                    minus_scores = scores_of[u - 1][0]
                minus_top = stream.tile([P, 2], F32, tag="minus_top", name="minus_top", bufs=8)
                scores_of[u] = (minus_scores, minus_top)
            return scores_of[u]

        def top_prev(u):
            minus_scores, minus_top = scores_tile(u)
            nc.vector.tensor_scalar(
                out=minus_scores[:, :CHUNK],
                in0=s_prev_of[u][:],
                scalar1=-1.0,
                scalar2=None,
                op0=ALU.mult,
                op1=ALU.min,
                accum_out=minus_top[:, 0:1],
            )

        def top_own(u):
            n, i = divmod(tile_and_head(u)[0], TILES)
            own = (i + 1) * P
            minus_scores, minus_top = scores_tile(u)
            s_own, first = s_own_of[u]
            nc.vector.tensor_scalar(
                out=minus_scores[:, place(u) : place(u) + own],
                in0=s_own[:, first : first + own],
                scalar1=-1.0,
                scalar2=(minus_top[:, 0:1] if n > 0 else None),
                op0=ALU.mult,
                op1=ALU.min,
                accum_out=minus_top[:, 1:2],
            )

        def exponential(u):
            j, h = tile_and_head(u)
            n, i = divmod(j, TILES)
            first = 0 if n > 0 else place(u)
            last = place(u) + (i + 1) * P
            minus_scores, minus_top = scores_of[u]
            if first_of_step(u):
                e = stream.tile([P, 2 * CHUNK], BF16, tag="e", name="e", bufs=3)
            else:
                e = e_of[u - 1]
            if i % 2 == 0:
                nc.gpsimd.memset(e[:, last : last + P].bitcast(mybir.dt.int32), 0)
            nc.scalar.activation(
                out=e[:, first:last],
                in_=minus_scores[:, first:last],
                func=ACT.Exp,
                bias=minus_top[:, 1:2],
                scale=-1.0,
                accum_out=den[:, j * NH + h : j * NH + h + 1],
            )
            e_of[u] = e

        def flip_e(u):
            n, i = divmod(tile_and_head(u)[0], TILES)
            j, h = tile_and_head(u)
            if first_of_step(u) and (i > 1 or h == 0):
                e_flip = psum.tile([P, TILES, P], F32, tag="e_flip", name="e_flip")
            else:
                e_flip = e_flip_of[u - 1]
            words = e_of[u][:].bitcast(F32)
            own = place(u) // (2 * P)
            for b in list(range(2 * n)) + list(range(own, own + i // 2 + 1)):
                nc.tensor.transpose(e_flip[:, b, :], words[:, b * P : (b + 1) * P], ident_f32[:])
            if i < 2 and h == 0:
                nc.tensor.transpose(e_flip[:, 2 + n, :], zeros[:], ident_f32[:])
            e_flip_of[u] = e_flip

        def grouped_of(j):
            return e_grouped[0 if j % TILES < 2 else 1 + j % 2]

        def regroup_e(u):
            j, h = tile_and_head(u)
            n, i = divmod(j, TILES)
            e_flip = e_flip_of[u]
            words = grouped_of(j)[:].rearrange("p r h q t -> p (r h q t)").bitcast(F32).rearrange("p (r h q u) -> p r h q u", r=2, h=NH, u=2)
            own = place(u) // (2 * P)
            if n > 0:
                nc.scalar.copy(out=words[:, :, h, :, :], in_=e_flip[:].rearrange("p (r u) q -> p r q u", r=2))
                return
            first = e_flip[:, own : own + 2, :] if i >= 2 else e_flip[:, own : 3 : 2 - own, :]
            nc.scalar.copy(out=words[:, 1, h, :, :], in_=first.rearrange("p u q -> p q u"))

        def regroup_e_pair(u):
            j, h = tile_and_head(u)
            words = grouped_of(j)[:, 1, h : h + 2, :, :].rearrange("p h q t -> p (h q t)").bitcast(F32).rearrange("p (h q u) -> p h q u", h=2, u=2)
            nc.scalar.copy(out=words, in_=e_flip_of[u][:].rearrange("p (h u) q -> p h q u", u=2))

        def slots_of(j):
            return slice(j, j + 1) if j < TILES else slice(2 * j - TILES, 2 * j - TILES + 2)

        def quantise_e(j):
            slots = slots_of(j)
            first = 1 if j < TILES else 0
            nc.vector.quantize_mx(
                out=e_codes[:, slots, :].rearrange("p s c -> p (s c)").bitcast(FP8X4),
                scales=e_scales[:, slots, :].rearrange("p s c -> p (s c)"),
                in_=grouped_of(j)[:, first:, :, :, :].rearrange("p r h q t -> p (r h q t)"),
            )

        def invert_den(n):
            cols = slice(n * TILES * NH, (n + 1) * TILES * NH)
            nc.vector.reciprocal(out=one_over_den[:, cols], in_=den[:, cols])

        def attend(j, heads, o):
            n = j // TILES
            slots = slots_of(j)
            for h in heads:
                cols = slice(h * DH, (h + 1) * DH)
                for slot in range(slots.start, slots.stop):
                    chunk = n - (slots.stop - 1 - slot)
                    nc.tensor.matmul_mx(
                        out=o[:, cols],
                        lhsT=e_codes[:, slot, cols].bitcast(FP8X4),
                        lhsT_scale=e_scales[:, slot, cols],
                        rhs=v_codes[:, chunk, cols].bitcast(FP8X4),
                        rhs_scale=v_scales[:, chunk, cols],
                        start=(slot == slots.start),
                        stop=(slot == slots.stop - 1),
                    )

        def divide(j, heads, o, o_sb, on_vector):
            cols = slice(heads[0] * DH, (heads[-1] + 1) * DH)
            recip = one_over_den[:, j * NH + heads[0] : j * NH + heads[-1] + 1]
            if on_vector:
                nc.vector.tensor_tensor(
                    out=o_sb,
                    in0=o[:, cols].rearrange("p (h d) -> p h d", d=DH),
                    in1=recip.unsqueeze(2).to_broadcast([P, len(heads), DH]),
                    op=ALU.mult,
                )
            else:
                for b, h in enumerate(heads):
                    nc.scalar.activation(
                        out=o_sb[:, b, :], in_=o[:, h * DH : (h + 1) * DH], func=ACT.Copy, scale=recip[:, b : b + 1]
                    )
            nc.sync.dma_start(out=out_rows[j * P : (j + 1) * P, cols], in_=o_sb.rearrange("p h d -> p (h d)"))

        def softmaxes_of(s):
            if -1 <= s <= 4:
                return (2 * s + 2, 2 * s + 3)
            if 5 <= s <= 12:
                return (s + 7,)
            if PASSES <= s < PASSES + 12:
                return (s + 4,)
            return ()

        def second(u):
            j, h = tile_and_head(u)
            return j == 2 and h % 2 == 1 or j == TILES

        qk_of = {
            -1: (2, (0, 1)),
            0: (3, (0, 1)),
            7: (4, (0,)),
            8: (4, (1,)),
            15: (5, (0, 1)),
            16: (7, (0, 1)),
            17: (6, (0, 1)),
        }

        load_wv(0)
        load_qk(0, 2)
        load_hidden(0, 1)
        load_qk(2, 4)
        for g in range(1, 4):
            load_hidden(g, 1)
            load_wv(g)
        load_wv(4)
        for n in range(2):
            v_rows_of[n] = stream.tile([P, TILES, W], BF16, tag="v_rows", name="v_rows")

        loads_of = {
            0: [lambda: load_hidden(4, 2)],
            1: [lambda: load_hidden(6, 2), lambda: load_qk(4, 6)],
            3: [lambda: load_hidden(8, 2)],
            5: [lambda: load_hidden(10, 2)],
            7: [lambda: load_hidden(12, 2)],
            9: [lambda: load_hidden(14, 2)],
            10: [lambda: load_half_tile(16), lambda: load_qk(6, 8)],
            11: [lambda: load_half_tile(18)],
            13: [lambda: load_half_tile(20)],
            15: [lambda: load_half_tile(22)],
            17: [lambda: load_half_tile(24)],
            19: [lambda: load_half_tile(26)],
            21: [lambda: load_half_tile(28)],
            23: [lambda: load_half_tile(30)],
        }

        regroup_wv(0)
        for j in range(2):
            room = psum.tile([P, 2 * NH, P], BF16, tag="bank%d" % j, name="qk_flip")
            flip_qk(j, (0, 1), room, (nc.scalar.copy, nc.vector.tensor_copy)[j])
        quantise_wv(0)
        for u in range(2):
            score_own(u)

        steps_of_a_tile = PASSES // PAIRS
        for s in range(-1, STEPS):
            before, now, after = softmaxes_of(s - 2), softmaxes_of(s), softmaxes_of(s + 1)
            for load in loads_of.get(s, []):
                load()
            if 0 <= s < PASSES - WV_AHEAD:
                load_wv(s + WV_AHEAD)
            for u in now:
                if tile_and_head(u)[0] >= TILES:
                    top_prev(u)
                elif not second(u):
                    top_own(u)
            if s <= 8 or s + 2 < STEPS:
                flip_hidden(s + 1 if s <= 8 else s + 2)
            for u in now:
                if tile_and_head(u)[0] >= TILES and not second(u):
                    top_own(u)
            if s in (23, 26, 29, 31):
                o_sb = stream.tile([P, NH, DH], F32, tag="o_sb", bufs=1)
                divide((23, 26, 29, 31).index(s), range(NH), o, o_sb[:], s < 31)
            for u in before:
                flip_e(u)
            if s in qk_of:
                j, which = qk_of[s]
                if s == -1:
                    room = psum.tile([P, 2 * NH, P], BF16, tag="bank2", name="qk_flip")
                elif s >= PASSES:
                    room = psum.tile([P, 2 * NH, P], BF16, tag="bank3", name="qk_flip")
                elif len(which) == 2:
                    room = psum.tile([P, 2 * NH, P], BF16, tag="e_flip", name="qk_flip")
                else:
                    room = e_flip_of[before[0]][:].rearrange("p b q -> p (b q)").bitcast(BF16).rearrange("p (b q) -> p b q", q=P)
                flip_qk(j, which, room, nc.vector.tensor_copy if s in (-1, 15,) else nc.scalar.copy)
            for u in now:
                if second(u):
                    score_own(u)
            if 0 < s + 1 < PASSES:
                regroup_wv(s + 1)
            if len(before) == 2 and tile_and_head(before[0])[0] == 2:
                regroup_e_pair(before[0])
            else:
                for u in before:
                    regroup_e(u)
            for u in now:
                if not second(u):
                    exponential(u)
            for u in now:
                if second(u):
                    top_own(u)
                    exponential(u)
            if 0 <= s + 1 < STEPS:
                quantise_hidden(s + 1)
            if 0 < s + 1 < PASSES:
                quantise_wv(s + 1)
            for u in before:
                if u % NH == NH - 1 and tile_and_head(u)[0] not in (2, 3, 4, 6):
                    quantise_e(tile_and_head(u)[0])
            if s in LATER_QUANTISED:
                quantise_e(LATER_QUANTISED[s])
            if s == 16:
                regroup_v(0, 0)
                regroup_v(0, 1)
            if s == 17:
                invert_den(0)
                quantise_v(0, 0)
                quantise_v(0, 1)
            if s >= 0:
                project(s)
            if s == 8:
                flip_hidden(s + 2)
            if s == PASSES - 1:
                round_v(2, nc.scalar.copy)
                round_v(0, nc.scalar.copy)
                round_v(3, nc.scalar.copy)
                round_v(1, nc.scalar.copy)
            if s >= PASSES and s in (22, 25, 28, 30):
                o = psum.tile([P, W], F32, tag="bank3", name="o")
                attend((22, 25, 28, 30).index(s), range(NH), o)
            if PASSES <= s < STEPS - 1 and s % steps_of_a_tile == steps_of_a_tile - 1:
                round_v(s // steps_of_a_tile, nc.scalar.copy)
            for u in after:
                if tile_and_head(u)[0] >= TILES:
                    score_prev(u, "s_own" if second(u) else "bank2")
                if not second(u):
                    score_own(u)

        last = 2 * TILES - 1
        half_cols = [slice(half * W // 2, (half + 1) * W // 2) for half in range(2)]
        nc.vector.tensor_copy(out=v_rows_of[1][:, TILES - 1, half_cols[0]], in_=accs[last][:, half_cols[0]])
        regroup_v(1, 0)
        quantise_v(1, 0)
        acc = psum.tile([P, W], F32, tag="bank0", name="acc_last")
        for g in range(PASSES):
            multiply(acc, STEPS - PASSES // PAIRS + g // PAIRS, g % PAIRS, g, half_cols[1])
        nc.vector.tensor_copy(out=v_rows_of[1][:, TILES - 1, half_cols[1]], in_=acc[:, half_cols[1]])
        invert_den(1)
        regroup_v(1, 1)
        quantise_v(1, 1)
        o_raw = stream.tile([P, LOAD_COLS], BF16, tag="x_raw", name="x_raw", bufs=4)
        o_parts = o_raw[:].bitcast(F32).rearrange("p (n h d) -> p n h d", h=2, d=DH)
        for half, tags in enumerate((("bank2", "bank3", "s_own", "e_flip"), ("bank1", "x_flip", "x_flip", "bank0"))):
            for n, (j, tag) in enumerate(zip(TILE_ORDER[TILES:], tags)):
                o = psum.tile([P, W], F32, tag=tag, name="o", bufs=(2 if tag == "x_flip" else 1))
                attend(j, HALVES[half], o)
                divide(j, HALVES[half], o, o_parts[:, half * TILES + n, :, :], n == 3 if half == 0 else n % 2 == 1)
